import numpy as np
import ml_dtypes


def mxq(x, axis, fmt="e4m3"):
    dtype, down = {"e4m3": (ml_dtypes.float8_e4m3fn, 7), "e5m2": (ml_dtypes.float8_e5m2, 14)}[fmt]
    v = np.moveaxis(np.asarray(x, np.float32).astype(ml_dtypes.bfloat16).astype(np.float64), axis, -1)
    blocks = v.reshape(v.shape[:-1] + (-1, 32))
    amax = np.abs(blocks).max(-1, keepdims=True)
    byte = np.maximum(np.where(amax > 0, np.frexp(amax)[1] - 1 + 127, 0) - down, 1)
    scale = np.exp2(byte - 127.0)
    codes = (blocks / scale).astype(np.float32).astype(dtype).astype(np.float64)
    return np.moveaxis((codes * scale).reshape(v.shape), -1, axis)


WIDE = False


def mx_kscale(k):
    if not WIDE:
        return np.ones(k)
    levels = np.array([10, -10, 5, -5, 0])
    a = np.random.permutation(np.resize(levels, k // 512 * 4)).reshape(k // 512, 4)
    idx = np.arange(k)
    return np.exp2(a[idx // 512, idx % 128 // 32])


BF16 = ml_dtypes.bfloat16


def bf(x):
    return np.asarray(x, np.float32).astype(BF16)


def f64(x):
    return np.asarray(x).astype(np.float64)


E2M1 = np.array([0.0, 0.5, 1.0, 1.5, 2.0, 3.0, 4.0, 6.0, -0.0, -0.5, -1.0, -1.5, -2.0, -3.0, -4.0, -6.0])


def pack_weight(w, fmt):
    k, n = w.shape
    w = f64(bf(w)).reshape(k // 32, 32, n)
    amax = np.abs(w).max(1)
    if fmt == "e4m3":
        byte = np.frexp(amax)[1] - 1 + 127 - 7
    else:
        mant, ex = np.frexp(amax / 6.0)
        byte = np.where(mant > 0.5, ex, ex - 1) + 127
    byte = np.clip(np.where(amax > 0, byte, 1), 1, 254)
    scaled = (w * np.exp2(127.0 - byte)[:, None, :]).reshape(k, n).astype(np.float32)
    by_word = np.ascontiguousarray(scaled.reshape(k // 512, 128, 4, n).transpose(0, 1, 3, 2))
    if fmt == "e4m3":
        words = by_word.astype(ml_dtypes.float8_e4m3fn).view(np.uint8)
    else:
        c = by_word.astype(ml_dtypes.float4_e2m1fn).view(np.uint8) & 0xF
        words = c[..., 0::2] | (c[..., 1::2] << 4)
    return np.ascontiguousarray(words), np.ascontiguousarray(byte.astype(np.uint8).reshape(k // 512, 16, n))


def unpack_weight(words, scales, fmt):
    g, p, n, _ = words.shape
    if fmt == "e4m3":
        vals = np.ascontiguousarray(words).view(ml_dtypes.float8_e4m3fn).astype(np.float64)
    else:
        nib = np.empty((g, p, n, 4), np.uint8)
        nib[..., 0::2] = words & 0xF
        nib[..., 1::2] = words >> 4
        vals = E2M1[nib]
    vals = vals * np.repeat(np.exp2(scales.astype(np.float64) - 127.0), 8, axis=1)[..., None]
    return vals.transpose(0, 1, 3, 2).reshape(g * 512, n)


B, N, D, H, R = 1, 128, 2048, 2, 32


def setup_inputs():
    s = mx_kscale(D)
    u = mx_kscale(D)
    b_scale = np.concatenate([np.full(H * D, 0.5 / np.sqrt(N)), np.full(H * D, 0.3)])
    x = bf(np.random.standard_normal((B, N, D)) * s)
    qkv_w_words, qkv_w_scales = pack_weight(np.random.standard_normal((D, 2 * H * D)) / np.sqrt(D) / s[:, None], "e4m3")
    qkv_b = bf(np.random.standard_normal(2 * H * D) * b_scale)
    lunchbox = bf(np.random.standard_normal((D, R)) * np.sqrt(D / (N * R)) * u[:, None])
    proj_w_words, proj_w_scales = pack_weight(np.random.standard_normal((H * D, D)) / np.sqrt(H * D) / np.tile(u, H)[:, None], "e4m3")
    proj_b = bf(np.random.standard_normal(D) * 0.3)
    return {"x": x,
            "qkv_w_words": qkv_w_words,
            "qkv_w_scales": qkv_w_scales,
            "qkv_b": qkv_b,
            "lunchbox": lunchbox,
            "proj_w_words": proj_w_words,
            "proj_w_scales": proj_w_scales,
            "proj_b": proj_b}


def reference(x, qkv_w_words, qkv_w_scales, qkv_b, lunchbox, proj_w_words, proj_w_scales, proj_b):
    scale = max(D, R) ** -0.5
    h = (mxq(f64(x), 2, "e4m3") @ unpack_weight(qkv_w_words, qkv_w_scales, "e4m3")) + f64(qkv_b)
    h = np.transpose(h, (0, 2, 1)).reshape(B, 2, H, D, N)
    q, v = h[:, 0], h[:, 1]
    attn = np.einsum('bhdn,dr->bhrd', q, f64(lunchbox)) * scale
    res = np.einsum('bhrd,bhdn->bhnd', attn, v)
    return (mxq(res.reshape(B, N, H * D), 2, "e4m3") @ unpack_weight(proj_w_words, proj_w_scales, "e4m3")) + f64(proj_b)

@@ -1,0 +1,285 @@
+import concourse.mybir as mybir
+from concourse.masks import make_identity
+
+FLOPS = 2 * 128 * 2048 * 8192 + 2 * 128 * 4096 * 2048
+
+BF16 = mybir.dt.bfloat16
+F32 = mybir.dt.float32
+I32 = mybir.dt.int32
+U8 = mybir.dt.uint8
+U32 = mybir.dt.uint32
+FP8X4 = mybir.dt.float8_e4m3fn_x4
+ADD = mybir.AluOpType.add
+MULT = mybir.AluOpType.mult
+
+P = 128
+SCALE = 2048.0 ** -0.5
+
+
+def tile_lunchboxmhsa_w_kernel(
+    tc, x, qkv_w_words, qkv_w_scales, qkv_b, lunchbox, proj_w_words, proj_w_scales, proj_b, out
+):
+    nc = tc.nc
+    x2 = x.flatten_outer_dims()
+    out2 = out.flatten_outer_dims()
+    qw = qkv_w_words.rearrange("g p n t -> g p (n t)").bitcast(I32)
+    qsc = qkv_w_scales.bitcast(I32)
+    pw = proj_w_words.rearrange("g p n t -> g p (n t)").bitcast(I32)
+    pw_by_g = pw.rearrange("(j g) p n -> g p j n", j=2)
+    psc = proj_w_scales.bitcast(I32)
+
+    with tc.tile_pool(name="const", bufs=1) as const, tc.tile_pool(name="wpool", bufs=1) as wpool, tc.tile_pool(
+        name="hpool", bufs=10
+    ) as hpool, tc.tile_pool(name="rpool", bufs=4) as rpool, tc.tile_pool(name="opool", bufs=4) as opool, tc.psum_pool(
+        name="psum", bufs=8
+    ) as psum:
+        qplanes = const.tile([P, 8192], U8, align_bytes=64)
+        pplanes = const.tile([P, 4096], U8, align_bytes=64)
+        brow = const.tile([P, 512], BF16)
+        x_sb = const.tile([P, 2048], BF16, align_bytes=64)
+        xg = const.tile([P, 2048], BF16, align_bytes=64)
+        xw = const.tile([P, 512], U32, align_bytes=64)
+        xs = const.tile([P, 512], U8, align_bytes=64)
+        ident = const.tile([P, P], F32)
+        identb = const.tile([P, P], BF16)
+        ones2 = const.tile([P, 2], F32)
+        bias_h = const.tile([P, 8192], BF16)
+        bias_o = const.tile([P, 2048], BF16)
+        lb = const.tile([P, 4, 128], BF16)
+        lsum = const.tile([P, 16], F32)
+        lscaled = const.tile([P, 16], F32)
+        cvec = const.tile([P, 32], F32)
+
+        nc.vector.memset(qplanes[:].bitcast(I32), 0)
+        nc.vector.memset(pplanes[:].bitcast(I32), 0)
+        nc.vector.memset(brow[:], 0.0)
+        make_identity(nc, ident[:])
+        nc.gpsimd.memset(ones2[:], 1.0)
+
+        nc.sync.dma_start(out=x_sb[:], in_=x2)
+        for quad in range(4):
+            nc.sync.dma_start(
+                out=qplanes[32 * quad : 32 * quad + 16, :].bitcast(I32), in_=qsc[:, 4 * quad : 4 * quad + 4, :]
+            )
+        for j in range(2):
+            for quad in range(4):
+                nc.sync.dma_start(
+                    out=pplanes[32 * quad : 32 * quad + 16, 2048 * j : 2048 * (j + 1)].bitcast(I32),
+                    in_=psc[4 * j : 4 * j + 4, 4 * quad : 4 * quad + 4, :],
+                )
+        nc.scalar.dma_start(out=brow[0:16, :], in_=qkv_b.rearrange("(r c) -> r c", c=512))
+        nc.scalar.dma_start(out=brow[16:20, :], in_=proj_b.rearrange("(r c) -> r c", c=512))
+        nc.scalar.dma_start(out=lb[:], in_=lunchbox.rearrange("(g p t) r -> p g (t r)", g=4, p=128, t=4))
+
+        nc.vector.tensor_copy(out=identb[:], in_=ident[:])
+
+        xwords = x_sb[:].bitcast(F32)
+        xgw = xg[:].bitcast(F32)
+        for a in range(2):
+            xt = psum.tile([P, 512], F32, name="xt", tag="bank")
+            for kl in range(2):
+                kx = 2 * a + kl
+                for u in range(2):
+                    s = 2 * kl + u
+                    nc.tensor.transpose(
+                        xt[:, 128 * s : 128 * (s + 1)], xwords[:, 256 * kx + u : 256 * (kx + 1) : 2], ident[:]
+                    )
+            nc.scalar.copy(
+                out=xgw[:, 512 * a : 512 * (a + 1)].rearrange("p (k n u) -> p k n u", k=2, u=2),
+                in_=xt[:].rearrange("p (k u n) -> p k n u", k=2, u=2),
+            )
+        nc.vector.quantize_mx(out=xw[:].bitcast(FP8X4), scales=xs[:], in_=xg[:])
+
+        for r in range(20):
+            bb = psum.tile([P, 512], F32, name="bb", tag="bank")
+            nc.tensor.matmul(
+                out=bb[:], lhsT=identb[:, r : r + 1].to_broadcast([P, P]), rhs=brow[:], start=True, stop=True
+            )
+            if r < 16:
+                nc.scalar.copy(
+                    out=bias_h[:, 512 * r : 512 * (r + 1)].rearrange("n (t p) -> n t p", t=4),
+                    in_=bb[:].rearrange("n (p t) -> n t p", t=4),
+                )
+            else:
+                nc.scalar.copy(out=bias_o[:, 512 * (r - 16) : 512 * (r - 15)], in_=bb[:])
+
+        nc.vector.tensor_reduce(
+            out=lsum[:], in_=lb[:].rearrange("p g (t r) -> p (g t) r", r=32), axis=mybir.AxisListType.X, op=ADD
+        )
+        nc.vector.tensor_scalar(out=lscaled[:], in0=lsum[:], scalar1=SCALE, scalar2=None, op0=MULT)
+
+        def mx1(acc, kx, c16, wbytes):
+            nc.tensor.matmul_mx(
+                out=acc[:],
+                lhsT=xw[:, 128 * kx : 128 * (kx + 1)].bitcast(FP8X4),
+                lhsT_scale=xs[:, 128 * kx : 128 * (kx + 1)],
+                rhs=wbytes.bitcast(FP8X4),
+                rhs_scale=qplanes[4 * kx : 128, 512 * c16 : 512 * (c16 + 1)],
+                start=(kx == 0),
+                stop=(kx == 3),
+            )
+
+        def add_bias(acc, c16):
+            hid = hpool.tile([P, 512], F32, name="hid", tag="hid")
+            nc.vector.tensor_tensor(
+                out=hid[:].rearrange("n (t p) -> n t p", t=4),
+                in0=acc[:].rearrange("n (p t) -> n t p", t=4),
+                in1=bias_h[:, 512 * c16 : 512 * (c16 + 1)].rearrange("n (t p) -> n t p", t=4),
+                op=ADD,
+            )
+            return hid
+
+        accq = []
+        for c in range(8):
+            acc = psum.tile([P, 512], F32, name="accq", tag="bank")
+            accq.append(acc)
+        for kx in range(4):
+            wt = wpool.tile([P, 16384], U8, name="wq", tag="w16", bufs=6, align_bytes=64)
+            nc.sync.dma_start(out=wt[:].bitcast(I32), in_=qw[kx][:, 0:4096])
+            for c in range(8):
+                mx1(accq[c], kx, c, wt[:, 2048 * c : 2048 * (c + 1)])
+
+        wv = []
+        for kx in range(3):
+            wt = wpool.tile([P, 16384], U8, name="wv", tag="w16", bufs=6, align_bytes=64)
+            nc.sync.dma_start(out=wt[:].bitcast(I32), in_=qw[kx][:, 4096:8192])
+            wv.append(wt)
+        wv3 = []
+        for a in range(2):
+            wt = wpool.tile([P, 8192], U8, name="wv3", tag="w8", bufs=3, align_bytes=64)
+            nc.sync.dma_start(
+                out=wt[:].bitcast(I32).rearrange("p (i d) -> p i d", i=2),
+                in_=qw[3][:, 4096:8192].rearrange("p (i d) -> p i d", i=2)[:, :, 1024 * a : 1024 * (a + 1)],
+            )
+            wv3.append(wt)
+        wp = []
+        for g in range(3):
+            wt = wpool.tile([P, 16384], U8, name="wp", tag="w16", bufs=6, align_bytes=64)
+            nc.sync.dma_start(out=wt[:].bitcast(I32).rearrange("p (j n) -> p j n", j=2), in_=pw_by_g[g])
+            wp.append(wt)
+        wp30 = wpool.tile([P, 8192], U8, name="wp30", tag="w8", bufs=3, align_bytes=64)
+        nc.sync.dma_start(out=wp30[:].bitcast(I32), in_=pw[3])
+        wp31 = []
+        for ct in range(4):
+            wt = wpool.tile([P, 2048], U8, name="wp31", tag="w2", bufs=4, align_bytes=64)
+            nc.sync.dma_start(out=wt[:].bitcast(I32), in_=pw[7][:, 512 * ct : 512 * (ct + 1)])
+            wp31.append(wt)
+
+        qsum = None
+        for c in range(8):
+            hq = add_bias(accq[c], c)
+            if qsum is None:
+                qsum = psum.tile([P, 512], F32, name="qsum", tag="bank")
+            for t in range(4):
+                blk = 4 * c + t
+                nc.tensor.matmul(
+                    out=qsum[:, 2 * blk : 2 * blk + 2],
+                    lhsT=hq[:, 128 * t : 128 * (t + 1)],
+                    rhs=ones2[:],
+                    start=True,
+                    stop=True,
+                )
+        nc.vector.tensor_tensor(
+            out=cvec[:].rearrange("p (i k) -> p i k", i=2),
+            in0=qsum[:, 0:64:2].rearrange("p (i k) -> p i k", i=2),
+            in1=lscaled[:].unsqueeze(1).to_broadcast([P, 2, 16]),
+            op=MULT,
+        )
+
+        accv = []
+        for c in range(8):
+            acc = psum.tile([P, 512], F32, name="accv", tag="bank")
+            accv.append(acc)
+        for kx in range(3):
+            for c in range(8):
+                mx1(accv[c], kx, 8 + c, wv[kx][:, 2048 * c : 2048 * (c + 1)])
+
+        def last_v_passes(a):
+            for gl in range(2):
+                for i in range(2):
+                    c = 4 * i + 2 * a + gl
+                    off = 4096 * i + 2048 * gl
+                    mx1(accv[c], 3, 8 + c, wv3[a][:, off : off + 2048])
+
+        hv = {}
+        tps = {}
+        rws = {}
+        rss = {}
+
+        def evac1(g):
+            for i in range(2):
+                hv[(i, g)] = add_bias(accv[4 * i + g], 8 + 4 * i + g)
+
+        def transposes(g):
+            for i in range(2):
+                tp = psum.tile([P, 512], F32, name="tp", tag="bank")
+                for t in range(4):
+                    nc.tensor.transpose(
+                        tp[:, 128 * t : 128 * (t + 1)], hv[(i, g)][:, 128 * t : 128 * (t + 1)], ident[:]
+                    )
+                tps[(i, g)] = tp
+
+        def evac2(g):
+            rg = rpool.tile([P, 2, 128, 4], BF16, name="rg", tag="rg", align_bytes=64)
+            for i in range(2):
+                c = 4 * i + g
+                nc.vector.tensor_tensor(
+                    out=rg[:, :, 64 * i : 64 * (i + 1), :],
+                    in0=tps[(i, g)][:].rearrange("p (t m j) -> p j m t", t=4, j=2),
+                    in1=cvec[:, 4 * c : 4 * c + 4].unsqueeze(1).unsqueeze(1).to_broadcast([P, 2, 64, 4]),
+                    op=MULT,
+                )
+            rw = rpool.tile([P, 256], U32, name="rw", tag="rw", align_bytes=64)
+            rs = rpool.tile([P, 256], U8, name="rs", tag="rs", align_bytes=64)
+            nc.vector.quantize_mx(out=rw[:].bitcast(FP8X4), scales=rs[:], in_=rg[:].rearrange("p j m t -> p (j m t)"))
+            rws[g] = rw
+            rss[g] = rs
+
+        acco = []
+
+        def mx2(ct, g, j, wbytes):
+            nc.tensor.matmul_mx(
+                out=acco[ct][:],
+                lhsT=rws[g][:, 128 * j : 128 * (j + 1)].bitcast(FP8X4),
+                lhsT_scale=rss[g][:, 128 * j : 128 * (j + 1)],
+                rhs=wbytes.bitcast(FP8X4),
+                rhs_scale=pplanes[4 * g : 128, 2048 * j + 512 * ct : 2048 * j + 512 * (ct + 1)],
+                start=(g == 0 and j == 0),
+                stop=(g == 3 and j == 1),
+            )
+
+        def proj(g):
+            for j in range(2):
+                for ct in range(4):
+                    off = 8192 * j + 2048 * ct
+                    mx2(ct, g, j, wp[g][:, off : off + 2048])
+
+        last_v_passes(0)
+        evac1(0)
+        evac1(1)
+        transposes(0)
+        last_v_passes(1)
+        transposes(1)
+        evac2(0)
+        evac1(2)
+        evac2(1)
+        transposes(2)
+        for ct in range(4):
+            acc = psum.tile([P, 512], F32, name="acco", tag="bank")
+            acco.append(acc)
+        proj(0)
+        evac1(3)
+        evac2(2)
+        transposes(3)
+        proj(1)
+        evac2(3)
+        proj(2)
+        for ct in range(4):
+            mx2(ct, 3, 0, wp30[:, 2048 * ct : 2048 * (ct + 1)])
+        for ct in range(4):
+            mx2(ct, 3, 1, wp31[ct][:])
+            o_sb = opool.tile([P, 512], F32, name="o_sb", tag="o_sb")
+            nc.vector.tensor_tensor(
+                out=o_sb[:], in0=acco[ct][:], in1=bias_o[:, 512 * ct : 512 * (ct + 1)], op=ADD
+            )
+            nc.sync.dma_start(out=out2[:, 512 * ct : 512 * (ct + 1)], in_=o_sb[:])

@@ -23,10 +23,10 @@ def tile_lunchboxmhsa_w_kernel(
     x2 = x.flatten_outer_dims()
     out2 = out.flatten_outer_dims()
     qw = qkv_w_words.rearrange("g p n t -> g p (n t)").bitcast(I32)
-    qsc = qkv_w_scales.bitcast(I32)
+    qsc = qkv_w_scales.bitcast(F32)
     pw = proj_w_words.rearrange("g p n t -> g p (n t)").bitcast(I32)
     pw_by_g = pw.rearrange("(j g) p n -> g p j n", j=2)
-    psc = proj_w_scales.bitcast(I32)
+    psc = proj_w_scales.bitcast(F32)
 
     with tc.tile_pool(name="const", bufs=1) as const, tc.tile_pool(name="wpool", bufs=1) as wpool, tc.tile_pool(
         name="hpool", bufs=10
@@ -43,7 +43,9 @@ def tile_lunchboxmhsa_w_kernel(
         ident = const.tile([P, P], F32)
         identb = const.tile([P, P], BF16)
         ones2 = const.tile([P, 2], F32)
-        bias_h = const.tile([P, 8192], BF16)
+        bias_v = const.tile([P, 4096], BF16)
+        bq128 = const.tile([P, 32], F32)
+        qtot = const.tile([P, 32], F32)
         bias_o = const.tile([P, 2048], BF16)
         lb = const.tile([P, 4, 128], BF16)
         lsum = const.tile([P, 16], F32)
@@ -58,13 +60,13 @@ def tile_lunchboxmhsa_w_kernel(
 
         nc.sync.dma_start(out=x_sb[:], in_=x2)
         for quad in range(4):
-            nc.sync.dma_start(
-                out=qplanes[32 * quad : 32 * quad + 16, :].bitcast(I32), in_=qsc[:, 4 * quad : 4 * quad + 4, :]
+            nc.gpsimd.dma_start(
+                out=qplanes[32 * quad : 32 * quad + 16, :].bitcast(F32), in_=qsc[:, 4 * quad : 4 * quad + 4, :]
             )
         for j in range(2):
             for quad in range(4):
-                nc.sync.dma_start(
-                    out=pplanes[32 * quad : 32 * quad + 16, 2048 * j : 2048 * (j + 1)].bitcast(I32),
+                nc.gpsimd.dma_start(
+                    out=pplanes[32 * quad : 32 * quad + 16, 2048 * j : 2048 * (j + 1)].bitcast(F32),
                     in_=psc[4 * j : 4 * j + 4, 4 * quad : 4 * quad + 4, :],
                 )
         nc.scalar.dma_start(out=brow[0:16, :], in_=qkv_b.rearrange("(r c) -> r c", c=512))
@@ -90,18 +92,33 @@ def tile_lunchboxmhsa_w_kernel(
             )
         nc.vector.quantize_mx(out=xw[:].bitcast(FP8X4), scales=xs[:], in_=xg[:])
 
-        for r in range(20):
+        bqp = psum.tile([P, 512], F32, name="bqp", tag="bank")
+        for t in range(4):
+            nc.tensor.matmul(
+                out=bqp[:, 32 * t : 32 * (t + 1)], lhsT=brow[:, t:512:4], rhs=identb[:, 0:32], start=True, stop=True
+            )
+        nc.vector.tensor_scalar(
+            out=bq128[:].rearrange("p (r t) -> p r t", t=4),
+            in0=bqp[:, 0:128].rearrange("p (t r) -> p r t", t=4)[:, 0:8, :],
+            scalar1=128.0,
+            scalar2=None,
+            op0=MULT,
+        )
+        for r in range(8, 20):
             bb = psum.tile([P, 512], F32, name="bb", tag="bank")
             nc.tensor.matmul(
                 out=bb[:], lhsT=identb[:, r : r + 1].to_broadcast([P, P]), rhs=brow[:], start=True, stop=True
             )
             if r < 16:
-                nc.scalar.copy(
-                    out=bias_h[:, 512 * r : 512 * (r + 1)].rearrange("n (t p) -> n t p", t=4),
-                    in_=bb[:].rearrange("n (p t) -> n t p", t=4),
-                )
+                dst = bias_v[:, 512 * (r - 8) : 512 * (r - 7)].rearrange("n (t p) -> n t p", t=4)
+                src = bb[:].rearrange("n (p t) -> n t p", t=4)
             else:
-                nc.scalar.copy(out=bias_o[:, 512 * (r - 16) : 512 * (r - 15)], in_=bb[:])
+                dst = bias_o[:, 512 * (r - 16) : 512 * (r - 15)]
+                src = bb[:]
+            if r % 2 == 0:
+                nc.scalar.copy(out=dst, in_=src)
+            else:
+                nc.vector.tensor_copy(out=dst, in_=src)
 
         nc.vector.tensor_reduce(
             out=lsum[:], in_=lb[:].rearrange("p g (t r) -> p (g t) r", r=32), axis=mybir.AxisListType.X, op=ADD
@@ -119,12 +136,12 @@ def tile_lunchboxmhsa_w_kernel(
                 stop=(kx == 3),
             )
 
-        def add_bias(acc, c16):
+        def add_bias(acc, c):
             hid = hpool.tile([P, 512], F32, name="hid", tag="hid")
             nc.vector.tensor_tensor(
                 out=hid[:].rearrange("n (t p) -> n t p", t=4),
                 in0=acc[:].rearrange("n (p t) -> n t p", t=4),
-                in1=bias_h[:, 512 * c16 : 512 * (c16 + 1)].rearrange("n (t p) -> n t p", t=4),
+                in1=bias_v[:, 512 * c : 512 * (c + 1)].rearrange("n (t p) -> n t p", t=4),
                 op=ADD,
             )
             return hid
@@ -167,7 +184,15 @@ def tile_lunchboxmhsa_w_kernel(
 
         qsum = None
         for c in range(8):
-            hq = add_bias(accq[c], c)
+            hq = hpool.tile([P, 512], F32, name="hq", tag="hid")
+            if c % 2 == 0:
+                nc.scalar.copy(
+                    out=hq[:].rearrange("n (t p) -> n t p", t=4), in_=accq[c][:].rearrange("n (p t) -> n t p", t=4)
+                )
+            else:
+                nc.vector.tensor_copy(
+                    out=hq[:].rearrange("n (t p) -> n t p", t=4), in_=accq[c][:].rearrange("n (p t) -> n t p", t=4)
+                )
             if qsum is None:
                 qsum = psum.tile([P, 512], F32, name="qsum", tag="bank")
             for t in range(4):
@@ -179,9 +204,10 @@ def tile_lunchboxmhsa_w_kernel(
                     start=True,
                     stop=True,
                 )
+        nc.vector.tensor_tensor(out=qtot[:], in0=qsum[:, 0:64:2], in1=bq128[:], op=ADD)
         nc.vector.tensor_tensor(
             out=cvec[:].rearrange("p (i k) -> p i k", i=2),
-            in0=qsum[:, 0:64:2].rearrange("p (i k) -> p i k", i=2),
+            in0=qtot[:].rearrange("p (i k) -> p i k", i=2),
             in1=lscaled[:].unsqueeze(1).to_broadcast([P, 2, 16]),
             op=MULT,
         )
@@ -208,7 +234,7 @@ def tile_lunchboxmhsa_w_kernel(
 
         def evac1(g):
             for i in range(2):
-                hv[(i, g)] = add_bias(accv[4 * i + g], 8 + 4 * i + g)
+                hv[(i, g)] = add_bias(accv[4 * i + g], 4 * i + g)
 
         def transposes(g):
             for i in range(2):

@@ -14,6 +14,7 @@ MULT = mybir.AluOpType.mult
 
 P = 128
 SCALE = 2048.0 ** -0.5
+RING = 16
 
 
 def tile_lunchboxmhsa_w_kernel(
@@ -23,16 +24,17 @@ def tile_lunchboxmhsa_w_kernel(
     x2 = x.flatten_outer_dims()
     out2 = out.flatten_outer_dims()
     qw = qkv_w_words.rearrange("g p n t -> g p (n t)").bitcast(I32)
-    qsc = qkv_w_scales.bitcast(F32)
+    qsc = qkv_w_scales.bitcast(I32)
     pw = proj_w_words.rearrange("g p n t -> g p (n t)").bitcast(I32)
-    pw_by_g = pw.rearrange("(j g) p n -> g p j n", j=2)
-    psc = proj_w_scales.bitcast(F32)
+    psc = proj_w_scales.bitcast(I32)
 
-    with tc.tile_pool(name="const", bufs=1) as const, tc.tile_pool(name="wpool", bufs=1) as wpool, tc.tile_pool(
-        name="hpool", bufs=10
-    ) as hpool, tc.tile_pool(name="rpool", bufs=4) as rpool, tc.tile_pool(name="opool", bufs=4) as opool, tc.psum_pool(
-        name="psum", bufs=8
-    ) as psum:
+    with tc.tile_pool(name="const", bufs=1) as const, tc.tile_pool(name="wpool", bufs=RING) as wpool, tc.tile_pool(
+        name="wlast", bufs=4
+    ) as wlast, tc.tile_pool(name="hpool", bufs=8) as hpool, tc.tile_pool(name="rpool", bufs=4) as rpool, tc.tile_pool(
+        name="opool", bufs=4
+    ) as opool, tc.psum_pool(name="pacc", bufs=4) as pacc, tc.psum_pool(
+        name="paux", bufs=4
+    ) as paux, tc.manual_schedule():
         qplanes = const.tile([P, 8192], U8, align_bytes=64)
         pplanes = const.tile([P, 4096], U8, align_bytes=64)
         brow = const.tile([P, 512], BF16)
@@ -44,41 +46,67 @@ def tile_lunchboxmhsa_w_kernel(
         identb = const.tile([P, P], BF16)
         ones2 = const.tile([P, 2], F32)
         bias_v = const.tile([P, 4096], BF16)
+        bias_o = const.tile([P, 2048], BF16)
         bq128 = const.tile([P, 32], F32)
         qtot = const.tile([P, 32], F32)
-        bias_o = const.tile([P, 2048], BF16)
         lb = const.tile([P, 4, 128], BF16)
         lsum = const.tile([P, 16], F32)
         lscaled = const.tile([P, 16], F32)
         cvec = const.tile([P, 32], F32)
 
+        slabs = {}
+        pieces = []
+
+        def load_slab(s):
+            if s == 23:
+                for ct in range(4):
+                    wt = wlast.tile([P, 2048], U8, name="wl", tag="wl", align_bytes=64)
+                    nc.sync.dma_start(out=wt[:].bitcast(I32), in_=pw[7][:, 512 * ct : 512 * (ct + 1)])
+                    pieces.append(wt)
+                return
+            wt = wpool.tile([P, 8192], U8, name="w", tag="w", align_bytes=64)
+            if s < 16:
+                grp = s // 4
+                nc.sync.dma_start(out=wt[:].bitcast(I32), in_=qw[s % 4][:, 2048 * grp : 2048 * (grp + 1)])
+            else:
+                g = (s - 16) // 2
+                j = (s - 16) % 2
+                nc.sync.dma_start(out=wt[:].bitcast(I32), in_=pw[4 * j + g])
+            slabs[s] = wt
+
+        def load_proj_scales(s):
+            j = s // 4
+            quad = s % 4
+            nc.sync.dma_start(
+                out=pplanes[32 * quad : 32 * quad + 16, 2048 * j : 2048 * (j + 1)].bitcast(I32),
+                in_=psc[4 * j : 4 * j + 4, 4 * quad : 4 * quad + 4, :],
+            )
+
+        nc.vector.memset(brow[:], 0.0)
         nc.vector.memset(qplanes[:].bitcast(I32), 0)
         nc.vector.memset(pplanes[:].bitcast(I32), 0)
-        nc.vector.memset(brow[:], 0.0)
         make_identity(nc, ident[:])
         nc.gpsimd.memset(ones2[:], 1.0)
 
         nc.sync.dma_start(out=x_sb[:], in_=x2)
-        for quad in range(4):
-            nc.gpsimd.dma_start(
-                out=qplanes[32 * quad : 32 * quad + 16, :].bitcast(F32), in_=qsc[:, 4 * quad : 4 * quad + 4, :]
-            )
-        for j in range(2):
-            for quad in range(4):
-                nc.gpsimd.dma_start(
-                    out=pplanes[32 * quad : 32 * quad + 16, 2048 * j : 2048 * (j + 1)].bitcast(F32),
-                    in_=psc[4 * j : 4 * j + 4, 4 * quad : 4 * quad + 4, :],
-                )
         nc.scalar.dma_start(out=brow[0:16, :], in_=qkv_b.rearrange("(r c) -> r c", c=512))
         nc.scalar.dma_start(out=brow[16:20, :], in_=proj_b.rearrange("(r c) -> r c", c=512))
         nc.scalar.dma_start(out=lb[:], in_=lunchbox.rearrange("(g p t) r -> p g (t r)", g=4, p=128, t=4))
+        for quad in range(4):
+            nc.sync.dma_start(
+                out=qplanes[32 * quad : 32 * quad + 16, :].bitcast(I32), in_=qsc[:, 4 * quad : 4 * quad + 4, :]
+            )
+        for s in range(RING):
+            load_slab(s)
+            if 4 <= s < 12:
+                load_proj_scales(s - 4)
 
         nc.vector.tensor_copy(out=identb[:], in_=ident[:])
 
         xwords = x_sb[:].bitcast(F32)
         xgw = xg[:].bitcast(F32)
         for a in range(2):
-            xt = psum.tile([P, 512], F32, name="xt", tag="bank")
+            xt = paux.tile([P, 512], F32, name="xt", tag="aux")
             for kl in range(2):
                 kx = 2 * a + kl
                 for u in range(2):
@@ -92,7 +120,7 @@ def tile_lunchboxmhsa_w_kernel(
             )
         nc.vector.quantize_mx(out=xw[:].bitcast(FP8X4), scales=xs[:], in_=xg[:])
 
-        bqp = psum.tile([P, 512], F32, name="bqp", tag="bank")
+        bqp = paux.tile([P, 512], F32, name="bqp", tag="aux")
         for t in range(4):
             nc.tensor.matmul(
                 out=bqp[:, 32 * t : 32 * (t + 1)], lhsT=brow[:, t:512:4], rhs=identb[:, 0:32], start=True, stop=True
@@ -105,7 +133,7 @@ def tile_lunchboxmhsa_w_kernel(
             op0=MULT,
         )
         for r in range(8, 20):
-            bb = psum.tile([P, 512], F32, name="bb", tag="bank")
+            bb = paux.tile([P, 512], F32, name="bb", tag="aux")
             nc.tensor.matmul(
                 out=bb[:], lhsT=identb[:, r : r + 1].to_broadcast([P, P]), rhs=brow[:], start=True, stop=True
             )
@@ -119,149 +147,111 @@ def tile_lunchboxmhsa_w_kernel(
                 nc.scalar.copy(out=dst, in_=src)
             else:
                 nc.vector.tensor_copy(out=dst, in_=src)
-
         nc.vector.tensor_reduce(
             out=lsum[:], in_=lb[:].rearrange("p g (t r) -> p (g t) r", r=32), axis=mybir.AxisListType.X, op=ADD
         )
         nc.vector.tensor_scalar(out=lscaled[:], in0=lsum[:], scalar1=SCALE, scalar2=None, op0=MULT)
 
-        def mx1(acc, kx, c16, wbytes):
-            nc.tensor.matmul_mx(
-                out=acc[:],
-                lhsT=xw[:, 128 * kx : 128 * (kx + 1)].bitcast(FP8X4),
-                lhsT_scale=xs[:, 128 * kx : 128 * (kx + 1)],
-                rhs=wbytes.bitcast(FP8X4),
-                rhs_scale=qplanes[4 * kx : 128, 512 * c16 : 512 * (c16 + 1)],
-                start=(kx == 0),
-                stop=(kx == 3),
-            )
+        accs = {}
+        hids = {}
+        qsums = {}
+        tps = {}
+        rgs = {}
+        rws = {}
+        rss = {}
+        acco = []
 
-        def add_bias(acc, c):
+        def passes(grp, kx):
+            s = 4 * grp + kx
+            for g in range(4):
+                if kx == 0:
+                    acc = pacc.tile([P, 512], F32, name="acc", tag="acc")
+                    accs[(grp, g)] = acc
+                c16 = 4 * grp + g
+                nc.tensor.matmul_mx(
+                    out=accs[(grp, g)][:],
+                    lhsT=xw[:, 128 * kx : 128 * (kx + 1)].bitcast(FP8X4),
+                    lhsT_scale=xs[:, 128 * kx : 128 * (kx + 1)],
+                    rhs=slabs[s][:, 2048 * g : 2048 * (g + 1)].bitcast(FP8X4),
+                    rhs_scale=qplanes[4 * kx : 128, 512 * c16 : 512 * (c16 + 1)],
+                    start=(kx == 0),
+                    stop=(kx == 3),
+                )
+            if s + RING < 24:
+                load_slab(s + RING)
+
+        def evac_q(i, g):
             hid = hpool.tile([P, 512], F32, name="hid", tag="hid")
-            nc.vector.tensor_tensor(
-                out=hid[:].rearrange("n (t p) -> n t p", t=4),
-                in0=acc[:].rearrange("n (p t) -> n t p", t=4),
-                in1=bias_v[:, 512 * c : 512 * (c + 1)].rearrange("n (t p) -> n t p", t=4),
-                op=ADD,
-            )
-            return hid
-
-        accq = []
-        for c in range(8):
-            acc = psum.tile([P, 512], F32, name="accq", tag="bank")
-            accq.append(acc)
-        for kx in range(4):
-            wt = wpool.tile([P, 16384], U8, name="wq", tag="w16", bufs=6, align_bytes=64)
-            nc.sync.dma_start(out=wt[:].bitcast(I32), in_=qw[kx][:, 0:4096])
-            for c in range(8):
-                mx1(accq[c], kx, c, wt[:, 2048 * c : 2048 * (c + 1)])
-
-        wv = []
-        for kx in range(3):
-            wt = wpool.tile([P, 16384], U8, name="wv", tag="w16", bufs=6, align_bytes=64)
-            nc.sync.dma_start(out=wt[:].bitcast(I32), in_=qw[kx][:, 4096:8192])
-            wv.append(wt)
-        wv3 = []
-        for a in range(2):
-            wt = wpool.tile([P, 8192], U8, name="wv3", tag="w8", bufs=3, align_bytes=64)
-            nc.sync.dma_start(
-                out=wt[:].bitcast(I32).rearrange("p (i d) -> p i d", i=2),
-                in_=qw[3][:, 4096:8192].rearrange("p (i d) -> p i d", i=2)[:, :, 1024 * a : 1024 * (a + 1)],
-            )
-            wv3.append(wt)
-        wp = []
-        for g in range(3):
-            wt = wpool.tile([P, 16384], U8, name="wp", tag="w16", bufs=6, align_bytes=64)
-            nc.sync.dma_start(out=wt[:].bitcast(I32).rearrange("p (j n) -> p j n", j=2), in_=pw_by_g[g])
-            wp.append(wt)
-        wp30 = wpool.tile([P, 8192], U8, name="wp30", tag="w8", bufs=3, align_bytes=64)
-        nc.sync.dma_start(out=wp30[:].bitcast(I32), in_=pw[3])
-        wp31 = []
-        for ct in range(4):
-            wt = wpool.tile([P, 2048], U8, name="wp31", tag="w2", bufs=4, align_bytes=64)
-            nc.sync.dma_start(out=wt[:].bitcast(I32), in_=pw[7][:, 512 * ct : 512 * (ct + 1)])
-            wp31.append(wt)
-
-        qsum = None
-        for c in range(8):
-            hq = hpool.tile([P, 512], F32, name="hq", tag="hid")
-            if c % 2 == 0:
-                nc.scalar.copy(
-                    out=hq[:].rearrange("n (t p) -> n t p", t=4), in_=accq[c][:].rearrange("n (p t) -> n t p", t=4)
-                )
+            dst = hid[:].rearrange("n (t p) -> n t p", t=4)
+            src = accs[(i, g)][:].rearrange("n (p t) -> n t p", t=4)
+            if g % 2 == 0:
+                nc.scalar.copy(out=dst, in_=src)
             else:
-                nc.vector.tensor_copy(
-                    out=hq[:].rearrange("n (t p) -> n t p", t=4), in_=accq[c][:].rearrange("n (p t) -> n t p", t=4)
-                )
-            if qsum is None:
-                qsum = psum.tile([P, 512], F32, name="qsum", tag="bank")
+                nc.vector.tensor_copy(out=dst, in_=src)
+            hids[(i, g)] = hid
+
+        def qsum_mm(i, g):
+            if g == 0:
+                qsum = paux.tile([P, 512], F32, name="qsum", tag="aux")
+                qsums[i] = qsum
             for t in range(4):
-                blk = 4 * c + t
+                blk = 4 * g + t
                 nc.tensor.matmul(
-                    out=qsum[:, 2 * blk : 2 * blk + 2],
-                    lhsT=hq[:, 128 * t : 128 * (t + 1)],
+                    out=qsums[i][:, 2 * blk : 2 * blk + 2],
+                    lhsT=hids[(i, g)][:, 128 * t : 128 * (t + 1)],
                     rhs=ones2[:],
                     start=True,
                     stop=True,
                 )
-        nc.vector.tensor_tensor(out=qtot[:], in0=qsum[:, 0:64:2], in1=bq128[:], op=ADD)
-        nc.vector.tensor_tensor(
-            out=cvec[:].rearrange("p (i k) -> p i k", i=2),
-            in0=qtot[:].rearrange("p (i k) -> p i k", i=2),
-            in1=lscaled[:].unsqueeze(1).to_broadcast([P, 2, 16]),
-            op=MULT,
-        )
 
-        accv = []
-        for c in range(8):
-            acc = psum.tile([P, 512], F32, name="accv", tag="bank")
-            accv.append(acc)
-        for kx in range(3):
-            for c in range(8):
-                mx1(accv[c], kx, 8 + c, wv[kx][:, 2048 * c : 2048 * (c + 1)])
+        def factor(i):
+            sl = slice(16 * i, 16 * (i + 1))
+            nc.vector.tensor_tensor(out=qtot[:, sl], in0=qsums[i][:, 0:32:2], in1=bq128[:, sl], op=ADD)
+            nc.vector.tensor_tensor(out=cvec[:, sl], in0=qtot[:, sl], in1=lscaled[:], op=MULT)
 
-        def last_v_passes(a):
-            for gl in range(2):
-                for i in range(2):
-                    c = 4 * i + 2 * a + gl
-                    off = 4096 * i + 2048 * gl
-                    mx1(accv[c], 3, 8 + c, wv3[a][:, off : off + 2048])
+        def evac1(i, g):
+            hid = hpool.tile([P, 512], F32, name="hid", tag="hid")
+            c = 4 * i + g
+            nc.vector.tensor_tensor(
+                out=hid[:].rearrange("n (t p) -> n t p", t=4),
+                in0=accs[(2 + i, g)][:].rearrange("n (p t) -> n t p", t=4),
+                in1=bias_v[:, 512 * c : 512 * (c + 1)].rearrange("n (t p) -> n t p", t=4),
+                op=ADD,
+            )
+            hids[(2 + i, g)] = hid
 
-        hv = {}
-        tps = {}
-        rws = {}
-        rss = {}
-
-        def evac1(g):
-            for i in range(2):
-                hv[(i, g)] = add_bias(accv[4 * i + g], 4 * i + g)
-
-        def transposes(g):
-            for i in range(2):
-                tp = psum.tile([P, 512], F32, name="tp", tag="bank")
-                for t in range(4):
-                    nc.tensor.transpose(
-                        tp[:, 128 * t : 128 * (t + 1)], hv[(i, g)][:, 128 * t : 128 * (t + 1)], ident[:]
-                    )
-                tps[(i, g)] = tp
-
-        def evac2(g):
-            rg = rpool.tile([P, 2, 128, 4], BF16, name="rg", tag="rg", align_bytes=64)
-            for i in range(2):
-                c = 4 * i + g
-                nc.vector.tensor_tensor(
-                    out=rg[:, :, 64 * i : 64 * (i + 1), :],
-                    in0=tps[(i, g)][:].rearrange("p (t m j) -> p j m t", t=4, j=2),
-                    in1=cvec[:, 4 * c : 4 * c + 4].unsqueeze(1).unsqueeze(1).to_broadcast([P, 2, 64, 4]),
-                    op=MULT,
+        def transposes(i, g):
+            tp = paux.tile([P, 512], F32, name="tp", tag="aux")
+            for t in range(4):
+                nc.tensor.transpose(
+                    tp[:, 128 * t : 128 * (t + 1)], hids[(2 + i, g)][:, 128 * t : 128 * (t + 1)], ident[:]
                 )
-            rw = rpool.tile([P, 256], U32, name="rw", tag="rw", align_bytes=64)
-            rs = rpool.tile([P, 256], U8, name="rs", tag="rs", align_bytes=64)
-            nc.vector.quantize_mx(out=rw[:].bitcast(FP8X4), scales=rs[:], in_=rg[:].rearrange("p j m t -> p (j m t)"))
-            rws[g] = rw
-            rss[g] = rs
+            tps[(i, g)] = tp
 
-        acco = []
+        def evac2(i, g):
+            if i == 0:
+                rg = rpool.tile([P, 2, 2, 64, 4], BF16, name="rg", tag="rg", align_bytes=64)
+                rw = rpool.tile([P, 256], U32, name="rw", tag="rw", align_bytes=64)
+                rs = rpool.tile([P, 256], U8, name="rs", tag="rs", align_bytes=64)
+                rgs[g] = rg
+                rws[g] = rw
+                rss[g] = rs
+            c = 4 * i + g
+            nc.vector.tensor_tensor(
+                out=rgs[g][:, :, i, :, :],
+                in0=tps[(i, g)][:].rearrange("p (t m j) -> p j m t", t=4, j=2),
+                in1=cvec[:, 4 * c : 4 * c + 4].unsqueeze(1).unsqueeze(1).to_broadcast([P, 2, 64, 4]),
+                op=MULT,
+            )
+
+        def quantise(i, g):
+            for j in range(2):
+                sl = slice(128 * j + 64 * i, 128 * j + 64 * (i + 1))
+                nc.vector.quantize_mx(
+                    out=rws[g][:, sl].bitcast(FP8X4),
+                    scales=rss[g][:, sl],
+                    in_=rgs[g][:, j, i, :, :].rearrange("p m t -> p (m t)"),
+                )
 
         def mx2(ct, g, j, wbytes):
             nc.tensor.matmul_mx(
@@ -274,36 +264,80 @@ def tile_lunchboxmhsa_w_kernel(
                 stop=(g == 3 and j == 1),
             )
 
-        def proj(g):
-            for j in range(2):
-                for ct in range(4):
-                    off = 8192 * j + 2048 * ct
-                    mx2(ct, g, j, wp[g][:, off : off + 2048])
+        def proj(g, j):
+            for ct in range(4):
+                if g == 0 and j == 0:
+                    acc = pacc.tile([P, 512], F32, name="acc", tag="acc")
+                    acco.append(acc)
+                mx2(ct, g, j, slabs[16 + 2 * g + j][:, 2048 * ct : 2048 * (ct + 1)])
 
-        last_v_passes(0)
-        evac1(0)
-        evac1(1)
-        transposes(0)
-        last_v_passes(1)
-        transposes(1)
-        evac2(0)
-        evac1(2)
-        evac2(1)
-        transposes(2)
+        for kx in range(4):
+            passes(0, kx)
+        for g in range(4):
+            evac_q(0, g)
+        passes(1, 0)
+        qsum_mm(0, 0)
+        qsum_mm(0, 1)
+        passes(1, 1)
+        qsum_mm(0, 2)
+        qsum_mm(0, 3)
+        factor(0)
+        passes(1, 2)
+        passes(1, 3)
+        for g in range(4):
+            evac_q(1, g)
+        passes(2, 0)
+        qsum_mm(1, 0)
+        qsum_mm(1, 1)
+        passes(2, 1)
+        qsum_mm(1, 2)
+        qsum_mm(1, 3)
+        factor(1)
+        passes(2, 2)
+        passes(2, 3)
+        for g in range(4):
+            evac1(0, g)
+        passes(3, 0)
+        transposes(0, 0)
+        transposes(0, 1)
+        evac2(0, 0)
+        evac2(0, 1)
+        quantise(0, 0)
+        quantise(0, 1)
+        passes(3, 1)
+        transposes(0, 2)
+        transposes(0, 3)
+        evac2(0, 2)
+        evac2(0, 3)
+        quantise(0, 2)
+        quantise(0, 3)
+        passes(3, 2)
+        passes(3, 3)
+        evac1(1, 0)
+        evac1(1, 1)
+        transposes(1, 0)
+        evac2(1, 0)
+        transposes(1, 1)
+        evac1(1, 2)
+        quantise(1, 0)
+        evac2(1, 1)
+        transposes(1, 2)
+        evac1(1, 3)
+        quantise(1, 1)
+        evac2(1, 2)
+        proj(0, 0)
+        proj(0, 1)
+        transposes(1, 3)
+        quantise(1, 2)
+        evac2(1, 3)
+        quantise(1, 3)
+        proj(1, 0)
+        proj(1, 1)
+        proj(2, 0)
+        proj(2, 1)
+        proj(3, 0)
         for ct in range(4):
-            acc = psum.tile([P, 512], F32, name="acco", tag="bank")
-            acco.append(acc)
-        proj(0)
-        evac1(3)
-        evac2(2)
-        transposes(3)
-        proj(1)
-        evac2(3)
-        proj(2)
-        for ct in range(4):
-            mx2(ct, 3, 0, wp30[:, 2048 * ct : 2048 * (ct + 1)])
-        for ct in range(4):
-            mx2(ct, 3, 1, wp31[ct][:])
+            mx2(ct, 3, 1, pieces[ct][:])
             o_sb = opool.tile([P, 512], F32, name="o_sb", tag="o_sb")
             nc.vector.tensor_tensor(
                 out=o_sb[:], in0=acco[ct][:], in1=bias_o[:, 512 * ct : 512 * (ct + 1)], op=ADD

@@ -24,9 +24,9 @@ def tile_lunchboxmhsa_w_kernel(
     x2 = x.flatten_outer_dims()
     out2 = out.flatten_outer_dims()
     qw = qkv_w_words.rearrange("g p n t -> g p (n t)").bitcast(I32)
-    qsc = qkv_w_scales.bitcast(I32)
+    qsc = qkv_w_scales.bitcast(F32)
     pw = proj_w_words.rearrange("g p n t -> g p (n t)").bitcast(I32)
-    psc = proj_w_scales.bitcast(I32)
+    psc = proj_w_scales.bitcast(F32)
 
     with tc.tile_pool(name="const", bufs=1) as const, tc.tile_pool(name="wpool", bufs=RING) as wpool, tc.tile_pool(
         name="wlast", bufs=4
@@ -77,8 +77,8 @@ def tile_lunchboxmhsa_w_kernel(
         def load_proj_scales(s):
             j = s // 4
             quad = s % 4
-            nc.sync.dma_start(
-                out=pplanes[32 * quad : 32 * quad + 16, 2048 * j : 2048 * (j + 1)].bitcast(I32),
+            nc.gpsimd.dma_start(
+                out=pplanes[32 * quad : 32 * quad + 16, 2048 * j : 2048 * (j + 1)].bitcast(F32),
                 in_=psc[4 * j : 4 * j + 4, 4 * quad : 4 * quad + 4, :],
             )
 
@@ -92,14 +92,16 @@ def tile_lunchboxmhsa_w_kernel(
         nc.scalar.dma_start(out=brow[0:16, :], in_=qkv_b.rearrange("(r c) -> r c", c=512))
         nc.scalar.dma_start(out=brow[16:20, :], in_=proj_b.rearrange("(r c) -> r c", c=512))
         nc.scalar.dma_start(out=lb[:], in_=lunchbox.rearrange("(g p t) r -> p g (t r)", g=4, p=128, t=4))
-        for quad in range(4):
-            nc.sync.dma_start(
-                out=qplanes[32 * quad : 32 * quad + 16, :].bitcast(I32), in_=qsc[:, 4 * quad : 4 * quad + 4, :]
-            )
+        for half in range(2):
+            for quad in range(4):
+                nc.gpsimd.dma_start(
+                    out=qplanes[32 * quad : 32 * quad + 16, 4096 * half : 4096 * (half + 1)].bitcast(F32),
+                    in_=qsc[:, 4 * quad : 4 * quad + 4, 1024 * half : 1024 * (half + 1)],
+                )
+        for s in range(8):
+            load_proj_scales(s)
         for s in range(RING):
             load_slab(s)
-            if 4 <= s < 12:
-                load_proj_scales(s - 4)
 
         nc.vector.tensor_copy(out=identb[:], in_=ident[:])
 

@@ -14,7 +14,6 @@ MULT = mybir.AluOpType.mult
 
 P = 128
 SCALE = 2048.0 ** -0.5
-RING = 16
 
 
 def tile_lunchboxmhsa_w_kernel(
@@ -25,10 +24,12 @@ def tile_lunchboxmhsa_w_kernel(
     out2 = out.flatten_outer_dims()
     qw = qkv_w_words.rearrange("g p n t -> g p (n t)").bitcast(I32)
     qsc = qkv_w_scales.bitcast(F32)
+    qw_by_p = qw.rearrange("k p n -> p k n")
     pw = proj_w_words.rearrange("g p n t -> g p (n t)").bitcast(I32)
+    pw_by_p = pw.rearrange("k p n -> p k n")
     psc = proj_w_scales.bitcast(F32)
 
-    with tc.tile_pool(name="const", bufs=1) as const, tc.tile_pool(name="wpool", bufs=RING) as wpool, tc.tile_pool(
+    with tc.tile_pool(name="const", bufs=1) as const, tc.tile_pool(name="wpool", bufs=4) as wpool, tc.tile_pool(
         name="wlast", bufs=4
     ) as wlast, tc.tile_pool(name="hpool", bufs=8) as hpool, tc.tile_pool(name="rpool", bufs=4) as rpool, tc.tile_pool(
         name="opool", bufs=4
@@ -57,22 +58,30 @@ def tile_lunchboxmhsa_w_kernel(
         slabs = {}
         pieces = []
 
-        def load_slab(s):
-            if s == 23:
-                for ct in range(4):
-                    wt = wlast.tile([P, 2048], U8, name="wl", tag="wl", align_bytes=64)
-                    nc.sync.dma_start(out=wt[:].bitcast(I32), in_=pw[7][:, 512 * ct : 512 * (ct + 1)])
-                    pieces.append(wt)
-                return
-            wt = wpool.tile([P, 8192], U8, name="w", tag="w", align_bytes=64)
-            if s < 16:
-                grp = s // 4
-                nc.sync.dma_start(out=wt[:].bitcast(I32), in_=qw[s % 4][:, 2048 * grp : 2048 * (grp + 1)])
-            else:
-                g = (s - 16) // 2
-                j = (s - 16) % 2
-                nc.sync.dma_start(out=wt[:].bitcast(I32), in_=pw[4 * j + g])
-            slabs[s] = wt
+        def load_group(grp):
+            wt = wpool.tile([P, 32768], U8, name="w", tag="w", align_bytes=64)
+            nc.sync.dma_start(
+                out=wt[:].bitcast(I32).rearrange("p (k n) -> p k n", k=4),
+                in_=qw_by_p[:, :, 2048 * grp : 2048 * (grp + 1)],
+            )
+            for kx in range(4):
+                slabs[4 * grp + kx] = wt[:, 8192 * kx : 8192 * (kx + 1)]
+
+        def load_proj(first, step, count):
+            wt = wpool.tile([P, 8192 * count], U8, name="w", tag="w", align_bytes=64)
+            nc.sync.dma_start(
+                out=wt[:].bitcast(I32).rearrange("p (k n) -> p k n", k=count),
+                in_=pw_by_p[:, first : first + step * (count - 1) + 1 : step, :],
+            )
+            for a in range(count):
+                k8 = first + step * a
+                slabs[16 + 2 * (k8 % 4) + k8 // 4] = wt[:, 8192 * a : 8192 * (a + 1)]
+
+        def load_pieces():
+            for ct in range(4):
+                wt = wlast.tile([P, 2048], U8, name="wl", tag="wl", align_bytes=64)
+                nc.sync.dma_start(out=wt[:].bitcast(I32), in_=pw[7][:, 512 * ct : 512 * (ct + 1)])
+                pieces.append(wt)
 
         def load_proj_scales(s):
             j = s // 4
@@ -100,8 +109,8 @@ def tile_lunchboxmhsa_w_kernel(
                 )
         for s in range(8):
             load_proj_scales(s)
-        for s in range(RING):
-            load_slab(s)
+        for grp in range(4):
+            load_group(grp)
 
         nc.vector.tensor_copy(out=identb[:], in_=ident[:])
 
@@ -163,24 +172,20 @@ def tile_lunchboxmhsa_w_kernel(
         rss = {}
         acco = []
 
-        def passes(grp, kx):
-            s = 4 * grp + kx
-            for g in range(4):
-                if kx == 0:
-                    acc = pacc.tile([P, 512], F32, name="acc", tag="acc")
-                    accs[(grp, g)] = acc
-                c16 = 4 * grp + g
+        def passes(grp, g):
+            acc = pacc.tile([P, 512], F32, name="acc", tag="acc")
+            accs[(grp, g)] = acc
+            c16 = 4 * grp + g
+            for kx in range(4):
                 nc.tensor.matmul_mx(
-                    out=accs[(grp, g)][:],
+                    out=acc[:],
                     lhsT=xw[:, 128 * kx : 128 * (kx + 1)].bitcast(FP8X4),
                     lhsT_scale=xs[:, 128 * kx : 128 * (kx + 1)],
-                    rhs=slabs[s][:, 2048 * g : 2048 * (g + 1)].bitcast(FP8X4),
+                    rhs=slabs[4 * grp + kx][:, 2048 * g : 2048 * (g + 1)].bitcast(FP8X4),
                     rhs_scale=qplanes[4 * kx : 128, 512 * c16 : 512 * (c16 + 1)],
                     start=(kx == 0),
                     stop=(kx == 3),
                 )
-            if s + RING < 24:
-                load_slab(s + RING)
 
         def evac_q(i, g):
             hid = hpool.tile([P, 512], F32, name="hid", tag="hid")
@@ -273,67 +278,54 @@ def tile_lunchboxmhsa_w_kernel(
                     acco.append(acc)
                 mx2(ct, g, j, slabs[16 + 2 * g + j][:, 2048 * ct : 2048 * (ct + 1)])
 
-        for kx in range(4):
-            passes(0, kx)
         for g in range(4):
+            passes(0, g)
             evac_q(0, g)
-        passes(1, 0)
-        qsum_mm(0, 0)
-        qsum_mm(0, 1)
-        passes(1, 1)
-        qsum_mm(0, 2)
-        qsum_mm(0, 3)
+        load_proj(0, 1, 2)
+        for g in range(4):
+            qsum_mm(0, g)
         factor(0)
-        passes(1, 2)
-        passes(1, 3)
         for g in range(4):
+            passes(1, g)
             evac_q(1, g)
-        passes(2, 0)
-        qsum_mm(1, 0)
-        qsum_mm(1, 1)
-        passes(2, 1)
-        qsum_mm(1, 2)
-        qsum_mm(1, 3)
-        factor(1)
-        passes(2, 2)
-        passes(2, 3)
+        load_proj(4, 1, 2)
         for g in range(4):
+            qsum_mm(1, g)
+        factor(1)
+        for g in range(4):
+            passes(2, g)
             evac1(0, g)
+        load_proj(2, 4, 2)
+        for g in range(4):
+            transposes(0, g)
+            evac2(0, g)
+        for g in range(4):
+            quantise(0, g)
         passes(3, 0)
-        transposes(0, 0)
-        transposes(0, 1)
-        evac2(0, 0)
-        evac2(0, 1)
-        quantise(0, 0)
-        quantise(0, 1)
-        passes(3, 1)
-        transposes(0, 2)
-        transposes(0, 3)
-        evac2(0, 2)
-        evac2(0, 3)
-        quantise(0, 2)
-        quantise(0, 3)
-        passes(3, 2)
-        passes(3, 3)
         evac1(1, 0)
+        passes(3, 1)
         evac1(1, 1)
         transposes(1, 0)
         evac2(1, 0)
-        transposes(1, 1)
+        passes(3, 2)
         evac1(1, 2)
         quantise(1, 0)
+        transposes(1, 1)
         evac2(1, 1)
-        transposes(1, 2)
+        passes(3, 3)
+        load_proj(3, 1, 1)
+        load_pieces()
         evac1(1, 3)
         quantise(1, 1)
+        transposes(1, 2)
         evac2(1, 2)
-        proj(0, 0)
-        proj(0, 1)
         transposes(1, 3)
         quantise(1, 2)
         evac2(1, 3)
         quantise(1, 3)
+        proj(0, 0)
         proj(1, 0)
+        proj(0, 1)
         proj(1, 1)
         proj(2, 0)
         proj(2, 1)

@@ -14,6 +14,7 @@ MULT = mybir.AluOpType.mult
 
 P = 128
 SCALE = 2048.0 ** -0.5
+RING = 16
 
 
 def tile_lunchboxmhsa_w_kernel(
@@ -24,18 +25,16 @@ def tile_lunchboxmhsa_w_kernel(
     out2 = out.flatten_outer_dims()
     qw = qkv_w_words.rearrange("g p n t -> g p (n t)").bitcast(I32)
     qsc = qkv_w_scales.bitcast(F32)
-    qw_by_p = qw.rearrange("k p n -> p k n")
     pw = proj_w_words.rearrange("g p n t -> g p (n t)").bitcast(I32)
-    pw_by_p = pw.rearrange("k p n -> p k n")
     psc = proj_w_scales.bitcast(F32)
 
-    with tc.tile_pool(name="const", bufs=1) as const, tc.tile_pool(name="wpool", bufs=4) as wpool, tc.tile_pool(
+    with tc.tile_pool(name="const", bufs=1) as const, tc.tile_pool(name="wpool", bufs=RING) as wpool, tc.tile_pool(
         name="wlast", bufs=4
     ) as wlast, tc.tile_pool(name="hpool", bufs=8) as hpool, tc.tile_pool(name="rpool", bufs=4) as rpool, tc.tile_pool(
         name="opool", bufs=4
     ) as opool, tc.psum_pool(name="pacc", bufs=4) as pacc, tc.psum_pool(
         name="paux", bufs=4
-    ) as paux, tc.manual_schedule():
+    ) as paux:
         qplanes = const.tile([P, 8192], U8, align_bytes=64)
         pplanes = const.tile([P, 4096], U8, align_bytes=64)
         brow = const.tile([P, 512], BF16)
@@ -58,30 +57,22 @@ def tile_lunchboxmhsa_w_kernel(
         slabs = {}
         pieces = []
 
-        def load_group(grp):
-            wt = wpool.tile([P, 32768], U8, name="w", tag="w", align_bytes=64)
-            nc.sync.dma_start(
-                out=wt[:].bitcast(I32).rearrange("p (k n) -> p k n", k=4),
-                in_=qw_by_p[:, :, 2048 * grp : 2048 * (grp + 1)],
-            )
-            for kx in range(4):
-                slabs[4 * grp + kx] = wt[:, 8192 * kx : 8192 * (kx + 1)]
-
-        def load_proj(first, step, count):
-            wt = wpool.tile([P, 8192 * count], U8, name="w", tag="w", align_bytes=64)
-            nc.sync.dma_start(
-                out=wt[:].bitcast(I32).rearrange("p (k n) -> p k n", k=count),
-                in_=pw_by_p[:, first : first + step * (count - 1) + 1 : step, :],
-            )
-            for a in range(count):
-                k8 = first + step * a
-                slabs[16 + 2 * (k8 % 4) + k8 // 4] = wt[:, 8192 * a : 8192 * (a + 1)]
-
-        def load_pieces():
-            for ct in range(4):
-                wt = wlast.tile([P, 2048], U8, name="wl", tag="wl", align_bytes=64)
-                nc.sync.dma_start(out=wt[:].bitcast(I32), in_=pw[7][:, 512 * ct : 512 * (ct + 1)])
-                pieces.append(wt)
+        def load_slab(s):
+            if s == 23:
+                for ct in range(4):
+                    wt = wlast.tile([P, 2048], U8, name="wl", tag="wl", align_bytes=64)
+                    nc.sync.dma_start(out=wt[:].bitcast(I32), in_=pw[7][:, 512 * ct : 512 * (ct + 1)])
+                    pieces.append(wt)
+                return
+            wt = wpool.tile([P, 8192], U8, name="w", tag="w", align_bytes=64)
+            if s < 16:
+                grp = s // 4
+                nc.sync.dma_start(out=wt[:].bitcast(I32), in_=qw[s % 4][:, 2048 * grp : 2048 * (grp + 1)])
+            else:
+                g = (s - 16) // 2
+                j = (s - 16) % 2
+                nc.sync.dma_start(out=wt[:].bitcast(I32), in_=pw[4 * j + g])
+            slabs[s] = wt
 
         def load_proj_scales(s):
             j = s // 4
@@ -109,8 +100,8 @@ def tile_lunchboxmhsa_w_kernel(
                 )
         for s in range(8):
             load_proj_scales(s)
-        for grp in range(4):
-            load_group(grp)
+        for s in range(RING):
+            load_slab(s)
 
         nc.vector.tensor_copy(out=identb[:], in_=ident[:])
 
@@ -172,20 +163,24 @@ def tile_lunchboxmhsa_w_kernel(
         rss = {}
         acco = []
 
-        def passes(grp, g):
-            acc = pacc.tile([P, 512], F32, name="acc", tag="acc")
-            accs[(grp, g)] = acc
-            c16 = 4 * grp + g
-            for kx in range(4):
+        def passes(grp, kx):
+            s = 4 * grp + kx
+            for g in range(4):
+                if kx == 0:
+                    acc = pacc.tile([P, 512], F32, name="acc", tag="acc")
+                    accs[(grp, g)] = acc
+                c16 = 4 * grp + g
                 nc.tensor.matmul_mx(
-                    out=acc[:],
+                    out=accs[(grp, g)][:],
                     lhsT=xw[:, 128 * kx : 128 * (kx + 1)].bitcast(FP8X4),
                     lhsT_scale=xs[:, 128 * kx : 128 * (kx + 1)],
-                    rhs=slabs[4 * grp + kx][:, 2048 * g : 2048 * (g + 1)].bitcast(FP8X4),
+                    rhs=slabs[s][:, 2048 * g : 2048 * (g + 1)].bitcast(FP8X4),
                     rhs_scale=qplanes[4 * kx : 128, 512 * c16 : 512 * (c16 + 1)],
                     start=(kx == 0),
                     stop=(kx == 3),
                 )
+            if s + RING < 24:
+                load_slab(s + RING)
 
         def evac_q(i, g):
             hid = hpool.tile([P, 512], F32, name="hid", tag="hid")
@@ -278,54 +273,67 @@ def tile_lunchboxmhsa_w_kernel(
                     acco.append(acc)
                 mx2(ct, g, j, slabs[16 + 2 * g + j][:, 2048 * ct : 2048 * (ct + 1)])
 
+        for kx in range(4):
+            passes(0, kx)
         for g in range(4):
-            passes(0, g)
             evac_q(0, g)
-        load_proj(0, 1, 2)
-        for g in range(4):
-            qsum_mm(0, g)
+        passes(1, 0)
+        qsum_mm(0, 0)
+        qsum_mm(0, 1)
+        passes(1, 1)
+        qsum_mm(0, 2)
+        qsum_mm(0, 3)
         factor(0)
+        passes(1, 2)
+        passes(1, 3)
         for g in range(4):
-            passes(1, g)
             evac_q(1, g)
-        load_proj(4, 1, 2)
-        for g in range(4):
-            qsum_mm(1, g)
+        passes(2, 0)
+        qsum_mm(1, 0)
+        qsum_mm(1, 1)
+        passes(2, 1)
+        qsum_mm(1, 2)
+        qsum_mm(1, 3)
         factor(1)
+        passes(2, 2)
+        passes(2, 3)
         for g in range(4):
-            passes(2, g)
             evac1(0, g)
-        load_proj(2, 4, 2)
-        for g in range(4):
-            transposes(0, g)
-            evac2(0, g)
-        for g in range(4):
-            quantise(0, g)
         passes(3, 0)
-        evac1(1, 0)
+        transposes(0, 0)
+        transposes(0, 1)
+        evac2(0, 0)
+        evac2(0, 1)
+        quantise(0, 0)
+        quantise(0, 1)
         passes(3, 1)
+        transposes(0, 2)
+        transposes(0, 3)
+        evac2(0, 2)
+        evac2(0, 3)
+        quantise(0, 2)
+        quantise(0, 3)
+        passes(3, 2)
+        passes(3, 3)
+        evac1(1, 0)
         evac1(1, 1)
         transposes(1, 0)
         evac2(1, 0)
-        passes(3, 2)
+        transposes(1, 1)
         evac1(1, 2)
         quantise(1, 0)
-        transposes(1, 1)
         evac2(1, 1)
-        passes(3, 3)
-        load_proj(3, 1, 1)
-        load_pieces()
+        transposes(1, 2)
         evac1(1, 3)
         quantise(1, 1)
-        transposes(1, 2)
         evac2(1, 2)
+        proj(0, 0)
+        proj(0, 1)
         transposes(1, 3)
         quantise(1, 2)
         evac2(1, 3)
         quantise(1, 3)
-        proj(0, 0)
         proj(1, 0)
-        proj(0, 1)
         proj(1, 1)
         proj(2, 0)
         proj(2, 1)

@@ -44,7 +44,7 @@ def tile_lunchboxmhsa_w_kernel(
         xs = const.tile([P, 512], U8, align_bytes=64)
         ident = const.tile([P, P], F32)
         identb = const.tile([P, P], BF16)
-        ones2 = const.tile([P, 2], F32)
+        qraw = const.tile([P, 32], F32)
         bias_v = const.tile([P, 4096], BF16)
         bias_o = const.tile([P, 2048], BF16)
         bq128 = const.tile([P, 32], F32)
@@ -86,7 +86,6 @@ def tile_lunchboxmhsa_w_kernel(
         nc.vector.memset(qplanes[:].bitcast(I32), 0)
         nc.vector.memset(pplanes[:].bitcast(I32), 0)
         make_identity(nc, ident[:])
-        nc.gpsimd.memset(ones2[:], 1.0)
 
         nc.sync.dma_start(out=x_sb[:], in_=x2)
         nc.scalar.dma_start(out=brow[0:16, :], in_=qkv_b.rearrange("(r c) -> r c", c=512))
@@ -156,7 +155,6 @@ def tile_lunchboxmhsa_w_kernel(
 
         accs = {}
         hids = {}
-        qsums = {}
         tps = {}
         rgs = {}
         rws = {}
@@ -193,22 +191,22 @@ def tile_lunchboxmhsa_w_kernel(
             hids[(i, g)] = hid
 
         def qsum_mm(i, g):
-            if g == 0:
-                qsum = paux.tile([P, 512], F32, name="qsum", tag="aux")
-                qsums[i] = qsum
+            qt = paux.tile([P, 512], F32, name="qt", tag="aux")
             for t in range(4):
-                blk = 4 * g + t
-                nc.tensor.matmul(
-                    out=qsums[i][:, 2 * blk : 2 * blk + 2],
-                    lhsT=hids[(i, g)][:, 128 * t : 128 * (t + 1)],
-                    rhs=ones2[:],
-                    start=True,
-                    stop=True,
+                nc.tensor.transpose(
+                    qt[:, 128 * t : 128 * (t + 1)], hids[(i, g)][:, 128 * t : 128 * (t + 1)], ident[:]
                 )
+            c = 4 * i + g
+            nc.vector.tensor_reduce(
+                out=qraw[:, 4 * c : 4 * c + 4],
+                in_=qt[:].rearrange("p (t n) -> p t n", t=4),
+                axis=mybir.AxisListType.X,
+                op=ADD,
+            )
 
         def factor(i):
             sl = slice(16 * i, 16 * (i + 1))
-            nc.vector.tensor_tensor(out=qtot[:, sl], in0=qsums[i][:, 0:32:2], in1=bq128[:, sl], op=ADD)
+            nc.vector.tensor_tensor(out=qtot[:, sl], in0=qraw[:, sl], in1=bq128[:, sl], op=ADD)
             nc.vector.tensor_tensor(out=cvec[:, sl], in0=qtot[:, sl], in1=lscaled[:], op=MULT)
 
         def evac1(i, g):

@@ -45,6 +45,7 @@ def tile_lunchboxmhsa_w_kernel(
         ident = const.tile([P, P], F32)
         identb = const.tile([P, P], BF16)
         qraw = const.tile([P, 32], F32)
+        warm = const.tile([P, 2], F32)
         bias_v = const.tile([P, 4096], BF16)
         bias_o = const.tile([P, 2048], BF16)
         bq128 = const.tile([P, 32], F32)
@@ -82,24 +83,34 @@ def tile_lunchboxmhsa_w_kernel(
                 in_=psc[4 * j : 4 * j + 4, 4 * quad : 4 * quad + 4, :],
             )
 
+        nc.gpsimd.memset(warm[:, 0:1], 0.0)
+        nc.scalar.copy(out=warm[:, 1:2], in_=warm[:, 0:1])
+        nc.vector.memset(qplanes[:, 0:2048].bitcast(I32), 0)
         nc.vector.memset(brow[:], 0.0)
-        nc.vector.memset(qplanes[:].bitcast(I32), 0)
+        nc.vector.memset(qplanes[:, 2048:8192].bitcast(I32), 0)
         nc.vector.memset(pplanes[:].bitcast(I32), 0)
         make_identity(nc, ident[:])
 
         nc.sync.dma_start(out=x_sb[:], in_=x2)
+        for quad in range(4):
+            nc.scalar.dma_start(
+                out=qplanes[32 * quad : 32 * quad + 16, 0:2048].bitcast(F32),
+                in_=qsc[:, 4 * quad : 4 * quad + 4, 0:512],
+            )
+        for s in range(3):
+            load_slab(s)
         nc.scalar.dma_start(out=brow[0:16, :], in_=qkv_b.rearrange("(r c) -> r c", c=512))
         nc.scalar.dma_start(out=brow[16:20, :], in_=proj_b.rearrange("(r c) -> r c", c=512))
         nc.scalar.dma_start(out=lb[:], in_=lunchbox.rearrange("(g p t) r -> p g (t r)", g=4, p=128, t=4))
-        for half in range(2):
+        for lo, hi in ((2048, 4096), (4096, 8192)):
             for quad in range(4):
                 nc.gpsimd.dma_start(
-                    out=qplanes[32 * quad : 32 * quad + 16, 4096 * half : 4096 * (half + 1)].bitcast(F32),
-                    in_=qsc[:, 4 * quad : 4 * quad + 4, 1024 * half : 1024 * (half + 1)],
+                    out=qplanes[32 * quad : 32 * quad + 16, lo:hi].bitcast(F32),
+                    in_=qsc[:, 4 * quad : 4 * quad + 4, lo // 4 : hi // 4],
                 )
         for s in range(8):
             load_proj_scales(s)
-        for s in range(RING):
+        for s in range(3, RING):
             load_slab(s)
 
         nc.vector.tensor_copy(out=identb[:], in_=ident[:])

@@ -44,7 +44,11 @@ def tile_lunchboxmhsa_w_kernel(
         xs = const.tile([P, 512], U8, align_bytes=64)
         ident = const.tile([P, P], F32)
         identb = const.tile([P, P], BF16)
-        qraw = const.tile([P, 32], F32)
+        qs = const.tile([P, P], F32)
+        qst = const.tile([P, P], F32)
+        qsel = const.tile([P, 512], F32)
+        mask4 = const.tile([P, 4], F32)
+        pick = const.tile([P, 32], F32)
         warm = const.tile([P, 2], F32)
         bias_v = const.tile([P, 4096], BF16)
         bias_o = const.tile([P, 2048], BF16)
@@ -114,6 +118,13 @@ def tile_lunchboxmhsa_w_kernel(
             load_slab(s)
 
         nc.vector.tensor_copy(out=identb[:], in_=ident[:])
+        nc.vector.memset(qs[:], 0.0)
+        nc.vector.tensor_reduce(
+            out=mask4[:], in_=ident[:].rearrange("c (x a) -> c a x", a=4), axis=mybir.AxisListType.X, op=ADD
+        )
+        nc.vector.tensor_reduce(
+            out=pick[:], in_=ident[:].rearrange("c (y z) -> c y z", z=4), axis=mybir.AxisListType.X, op=ADD
+        )
 
         xwords = x_sb[:].bitcast(F32)
         xgw = xg[:].bitcast(F32)
@@ -191,34 +202,55 @@ def tile_lunchboxmhsa_w_kernel(
             if s + RING < 24:
                 load_slab(s + RING)
 
-        def evac_q(i, g):
-            hid = hpool.tile([P, 512], F32, name="hid", tag="hid")
-            dst = hid[:].rearrange("n (t p) -> n t p", t=4)
-            src = accs[(i, g)][:].rearrange("n (p t) -> n t p", t=4)
-            if g % 2 == 0:
-                nc.scalar.copy(out=dst, in_=src)
-            else:
-                nc.vector.tensor_copy(out=dst, in_=src)
-            hids[(i, g)] = hid
-
-        def qsum_mm(i, g):
-            qt = paux.tile([P, 512], F32, name="qt", tag="aux")
-            for t in range(4):
-                nc.tensor.transpose(
-                    qt[:, 128 * t : 128 * (t + 1)], hids[(i, g)][:, 128 * t : 128 * (t + 1)], ident[:]
-                )
-            c = 4 * i + g
+        def q_tile(i, g):
+            acc = pacc.tile([P, 512], F32, name="acc", tag="acc")
+            c16 = 4 * i + g
+            for u in range(4):
+                for kx in range(4):
+                    nc.tensor.matmul_mx(
+                        out=acc[:, 128 * u : 128 * (u + 1)],
+                        lhsT=slabs[4 * i + kx][:, 2048 * g + 512 * u : 2048 * g + 512 * (u + 1)].bitcast(FP8X4),
+                        lhsT_scale=qplanes[4 * kx : 128, 512 * c16 + 128 * u : 512 * c16 + 128 * (u + 1)],
+                        rhs=xw[:, 128 * kx : 128 * (kx + 1)].bitcast(FP8X4),
+                        rhs_scale=xs[:, 128 * kx : 128 * (kx + 1)],
+                        start=(kx == 0),
+                        stop=(kx == 3),
+                    )
             nc.vector.tensor_reduce(
-                out=qraw[:, 4 * c : 4 * c + 4],
-                in_=qt[:].rearrange("p (t n) -> p t n", t=4),
+                out=qs[:, 4 * c16 : 4 * c16 + 4],
+                in_=acc[:].rearrange("p (u n) -> p u n", u=4),
                 axis=mybir.AxisListType.X,
                 op=ADD,
             )
 
-        def factor(i):
-            sl = slice(16 * i, 16 * (i + 1))
-            nc.vector.tensor_tensor(out=qtot[:, sl], in0=qraw[:, sl], in1=bq128[:, sl], op=ADD)
-            nc.vector.tensor_tensor(out=cvec[:, sl], in0=qtot[:, sl], in1=lscaled[:], op=MULT)
+        def factor():
+            t1 = paux.tile([P, 512], F32, name="t1", tag="aux")
+            nc.tensor.transpose(t1[:, 0:128], qs[:], ident[:])
+            nc.scalar.copy(out=qst[:], in_=t1[:, 0:128])
+            nc.vector.tensor_tensor(
+                out=qsel[:].rearrange("c (t a b) -> c t a b", t=4, a=4),
+                in0=qst[:].rearrange("c (b t) -> c t b", t=4).unsqueeze(2).to_broadcast([P, 4, 4, 32]),
+                in1=mask4[:].unsqueeze(1).unsqueeze(3).to_broadcast([P, 4, 4, 32]),
+                op=MULT,
+            )
+            s2 = paux.tile([P, 512], F32, name="s2", tag="aux")
+            for t in range(4):
+                nc.tensor.matmul(
+                    out=s2[:, 8 * t : 8 * (t + 1)],
+                    lhsT=qsel[:, 128 * t : 128 * (t + 1)],
+                    rhs=pick[:, 0:8],
+                    start=True,
+                    stop=True,
+                )
+            nc.vector.tensor_tensor(
+                out=qtot[:].rearrange("p (y t) -> p y t", t=4),
+                in0=s2[:, 0:32].rearrange("p (t y) -> p y t", t=4),
+                in1=bq128[:].rearrange("p (y t) -> p y t", t=4),
+                op=ADD,
+            )
+            for i in range(2):
+                sl = slice(16 * i, 16 * (i + 1))
+                nc.vector.tensor_tensor(out=cvec[:, sl], in0=qtot[:, sl], in1=lscaled[:], op=MULT)
 
         def evac1(i, g):
             hid = hpool.tile([P, 512], F32, name="hid", tag="hid")
@@ -282,30 +314,14 @@ def tile_lunchboxmhsa_w_kernel(
                     acco.append(acc)
                 mx2(ct, g, j, slabs[16 + 2 * g + j][:, 2048 * ct : 2048 * (ct + 1)])
 
+        for i in range(2):
+            for g in range(4):
+                q_tile(i, g)
+            for kx in range(4):
+                load_slab(4 * i + kx + RING)
+        factor()
         for kx in range(4):
-            passes(0, kx)
-        for g in range(4):
-            evac_q(0, g)
-        passes(1, 0)
-        qsum_mm(0, 0)
-        qsum_mm(0, 1)
-        passes(1, 1)
-        qsum_mm(0, 2)
-        qsum_mm(0, 3)
-        factor(0)
-        passes(1, 2)
-        passes(1, 3)
-        for g in range(4):
-            evac_q(1, g)
-        passes(2, 0)
-        qsum_mm(1, 0)
-        qsum_mm(1, 1)
-        passes(2, 1)
-        qsum_mm(1, 2)
-        qsum_mm(1, 3)
-        factor(1)
-        passes(2, 2)
-        passes(2, 3)
+            passes(2, kx)
         for g in range(4):
             evac1(0, g)
         passes(3, 0)

@@ -106,7 +106,7 @@ def tile_lunchboxmhsa_w_kernel(
         nc.scalar.dma_start(out=brow[0:16, :], in_=qkv_b.rearrange("(r c) -> r c", c=512))
         nc.scalar.dma_start(out=brow[16:20, :], in_=proj_b.rearrange("(r c) -> r c", c=512))
         nc.scalar.dma_start(out=lb[:], in_=lunchbox.rearrange("(g p t) r -> p g (t r)", g=4, p=128, t=4))
-        for lo, hi in ((2048, 4096), (4096, 8192)):
+        for lo, hi in ((2048, 8192),):
             for quad in range(4):
                 nc.gpsimd.dma_start(
                     out=qplanes[32 * quad : 32 * quad + 16, lo:hi].bitcast(F32),

@@ -61,16 +61,29 @@ def tile_lunchboxmhsa_w_kernel(
 
         slabs = {}
         pieces = []
+        late = []
 
         def load_slab(s):
             if s == 23:
                 for ct in range(4):
                     wt = wlast.tile([P, 2048], U8, name="wl", tag="wl", align_bytes=64)
-                    nc.sync.dma_start(out=wt[:].bitcast(I32), in_=pw[7][:, 512 * ct : 512 * (ct + 1)])
                     pieces.append(wt)
+                for ct in range(3):
+                    nc.sync.dma_start(out=pieces[ct][:].bitcast(I32), in_=pw[7][:, 512 * ct : 512 * (ct + 1)])
+                for wt, idx in late:
+                    nc.sync.dma_start(out=wt[:, 6144:8192].bitcast(I32), in_=pw[idx][:, 1536:2048])
+                for h in range(2):
+                    nc.sync.dma_start(
+                        out=pieces[3][:, 1024 * h : 1024 * (h + 1)].bitcast(I32),
+                        in_=pw[7][:, 1536 + 256 * h : 1536 + 256 * (h + 1)],
+                    )
                 return
             wt = wpool.tile([P, 8192], U8, name="w", tag="w", align_bytes=64)
-            if s < 16:
+            if s in (21, 22):
+                idx = 4 * ((s - 16) % 2) + (s - 16) // 2
+                nc.sync.dma_start(out=wt[:, 0:6144].bitcast(I32), in_=pw[idx][:, 0:1536])
+                late.append((wt, idx))
+            elif s < 16:
                 grp = s // 4
                 nc.sync.dma_start(out=wt[:].bitcast(I32), in_=qw[s % 4][:, 2048 * grp : 2048 * (grp + 1)])
             else:
@@ -307,8 +320,21 @@ def tile_lunchboxmhsa_w_kernel(
                 stop=(g == 3 and j == 1),
             )
 
-        def proj(g, j):
-            for ct in range(4):
+        accd = []
+
+        def mxd(g, j, wbytes, h):
+            nc.tensor.matmul_mx(
+                out=accd[h][:, 0:256],
+                lhsT=rws[g][:, 128 * j : 128 * (j + 1)].bitcast(FP8X4),
+                lhsT_scale=rss[g][:, 128 * j : 128 * (j + 1)],
+                rhs=wbytes.bitcast(FP8X4),
+                rhs_scale=pplanes[4 * g : 128, 2048 * j + 1536 + 256 * h : 2048 * j + 1536 + 256 * (h + 1)],
+                start=(g == 0 and j == 0),
+                stop=(g == 3 and j == 1),
+            )
+
+        def proj(g, j, tiles=3):
+            for ct in range(tiles):
                 if g == 0 and j == 0:
                     acc = pacc.tile([P, 512], F32, name="acc", tag="acc")
                     acco.append(acc)
@@ -361,12 +387,27 @@ def tile_lunchboxmhsa_w_kernel(
         proj(1, 0)
         proj(1, 1)
         proj(2, 0)
+        d0 = pacc.tile([P, 512], F32, name="acc", tag="acc")
+        d1 = paux.tile([P, 512], F32, name="d1", tag="aux")
+        accd.append(d0)
+        accd.append(d1)
+        for g, j in ((0, 0), (0, 1), (1, 0), (1, 1), (2, 0)):
+            for h in range(2):
+                mxd(g, j, slabs[16 + 2 * g + j][:, 6144 + 1024 * h : 6144 + 1024 * (h + 1)], h)
         proj(2, 1)
         proj(3, 0)
-        for ct in range(4):
-            mx2(ct, 3, 1, pieces[ct][:])
+
+        def finish(acc, c0, n):
             o_sb = opool.tile([P, 512], F32, name="o_sb", tag="o_sb")
-            nc.vector.tensor_tensor(
-                out=o_sb[:], in0=acco[ct][:], in1=bias_o[:, 512 * ct : 512 * (ct + 1)], op=ADD
-            )
-            nc.sync.dma_start(out=out2[:, 512 * ct : 512 * (ct + 1)], in_=o_sb[:])
+            nc.vector.tensor_tensor(out=o_sb[:, 0:n], in0=acc[:, 0:n], in1=bias_o[:, c0 : c0 + n], op=ADD)
+            nc.sync.dma_start(out=out2[:, c0 : c0 + n], in_=o_sb[:, 0:n])
+
+        for ct in range(3):
+            mx2(ct, 3, 1, pieces[ct][:])
+            finish(acco[ct], 512 * ct, 512)
+        for g, j in ((2, 1), (3, 0)):
+            for h in range(2):
+                mxd(g, j, slabs[16 + 2 * g + j][:, 6144 + 1024 * h : 6144 + 1024 * (h + 1)], h)
+        for h in range(2):
+            mxd(3, 1, pieces[3][:, 1024 * h : 1024 * (h + 1)], h)
+            finish(accd[h], 1536 + 256 * h, 256)

@@ -119,7 +119,7 @@ def tile_lunchboxmhsa_w_kernel(
         nc.scalar.dma_start(out=brow[0:16, :], in_=qkv_b.rearrange("(r c) -> r c", c=512))
         nc.scalar.dma_start(out=brow[16:20, :], in_=proj_b.rearrange("(r c) -> r c", c=512))
         nc.scalar.dma_start(out=lb[:], in_=lunchbox.rearrange("(g p t) r -> p g (t r)", g=4, p=128, t=4))
-        for lo, hi in ((2048, 8192),):
+        for lo, hi in ((2048, 4096), (4096, 8192)):
             for quad in range(4):
                 nc.gpsimd.dma_start(
                     out=qplanes[32 * quad : 32 * quad + 16, lo:hi].bitcast(F32),

import concourse.mybir as mybir
from concourse.masks import make_identity

FLOPS = 2 * 128 * 2048 * 8192 + 2 * 128 * 4096 * 2048

BF16 = mybir.dt.bfloat16
F32 = mybir.dt.float32
I32 = mybir.dt.int32
U8 = mybir.dt.uint8
U32 = mybir.dt.uint32
FP8X4 = mybir.dt.float8_e4m3fn_x4
ADD = mybir.AluOpType.add
MULT = mybir.AluOpType.mult

P = 128
SCALE = 2048.0 ** -0.5
RING = 16


def tile_lunchboxmhsa_w_kernel(
    tc, x, qkv_w_words, qkv_w_scales, qkv_b, lunchbox, proj_w_words, proj_w_scales, proj_b, out
):
    nc = tc.nc
    x2 = x.flatten_outer_dims()
    out2 = out.flatten_outer_dims()
    qw = qkv_w_words.rearrange("g p n t -> g p (n t)").bitcast(I32)
    qsc = qkv_w_scales.bitcast(F32)
    pw = proj_w_words.rearrange("g p n t -> g p (n t)").bitcast(I32)
    psc = proj_w_scales.bitcast(F32)

    with tc.tile_pool(name="const", bufs=1) as const, tc.tile_pool(name="wpool", bufs=RING) as wpool, tc.tile_pool(
        name="wlast", bufs=4
    ) as wlast, tc.tile_pool(name="hpool", bufs=8) as hpool, tc.tile_pool(name="rpool", bufs=4) as rpool, tc.tile_pool(
        name="opool", bufs=4
    ) as opool, tc.psum_pool(name="pacc", bufs=4) as pacc, tc.psum_pool(
        name="paux", bufs=4
    ) as paux:
        qplanes = const.tile([P, 8192], U8, align_bytes=64)
        pplanes = const.tile([P, 4096], U8, align_bytes=64)
        brow = const.tile([P, 512], BF16)
        x_sb = const.tile([P, 2048], BF16, align_bytes=64)
        xg = const.tile([P, 2048], BF16, align_bytes=64)
        xw = const.tile([P, 512], U32, align_bytes=64)
        xs = const.tile([P, 512], U8, align_bytes=64)
        ident = const.tile([P, P], F32)
        identb = const.tile([P, P], BF16)
        qs = const.tile([P, P], F32)
        qst = const.tile([P, P], F32)
        qsel = const.tile([P, 512], F32)
        mask4 = const.tile([P, 4], F32)
        pick = const.tile([P, 32], F32)
        warm = const.tile([P, 2], F32)
        bias_v = const.tile([P, 4096], BF16)
        bias_o = const.tile([P, 2048], BF16)
        bq128 = const.tile([P, 32], F32)
        qtot = const.tile([P, 32], F32)
        lb = const.tile([P, 4, 128], BF16)
        lsum = const.tile([P, 16], F32)
        lscaled = const.tile([P, 16], F32)
        cvec = const.tile([P, 32], F32)

        slabs = {}
        pieces = []
        late = []

        def load_slab(s):
            if s == 23:
                for ct in range(4):
                    wt = wlast.tile([P, 2048], U8, name="wl", tag="wl", align_bytes=64)
                    pieces.append(wt)
                for ct in range(3):
                    nc.sync.dma_start(out=pieces[ct][:].bitcast(I32), in_=pw[7][:, 512 * ct : 512 * (ct + 1)])
                for wt, idx in late:
                    nc.sync.dma_start(out=wt[:, 6144:8192].bitcast(I32), in_=pw[idx][:, 1536:2048])
                for h in range(2):
                    nc.sync.dma_start(
                        out=pieces[3][:, 1024 * h : 1024 * (h + 1)].bitcast(I32),
                        in_=pw[7][:, 1536 + 256 * h : 1536 + 256 * (h + 1)],
                    )
                return
            wt = wpool.tile([P, 8192], U8, name="w", tag="w", align_bytes=64)
            if s in (21, 22):
                idx = 4 * ((s - 16) % 2) + (s - 16) // 2
                nc.sync.dma_start(out=wt[:, 0:6144].bitcast(I32), in_=pw[idx][:, 0:1536])
                late.append((wt, idx))
            elif s < 16:
                grp = s // 4
                nc.sync.dma_start(out=wt[:].bitcast(I32), in_=qw[s % 4][:, 2048 * grp : 2048 * (grp + 1)])
            else:
                g = (s - 16) // 2
                j = (s - 16) % 2
                nc.sync.dma_start(out=wt[:].bitcast(I32), in_=pw[4 * j + g])
            slabs[s] = wt

        def load_proj_scales(s):
            j = s // 4
            quad = s % 4
            nc.gpsimd.dma_start(
                out=pplanes[32 * quad : 32 * quad + 16, 2048 * j : 2048 * (j + 1)].bitcast(F32),
                in_=psc[4 * j : 4 * j + 4, 4 * quad : 4 * quad + 4, :],
            )

        nc.gpsimd.memset(warm[:, 0:1], 0.0)
        nc.scalar.copy(out=warm[:, 1:2], in_=warm[:, 0:1])
        nc.vector.memset(qplanes[:, 0:2048].bitcast(I32), 0)
        nc.vector.memset(brow[:], 0.0)
        nc.vector.memset(qplanes[:, 2048:8192].bitcast(I32), 0)
        nc.vector.memset(pplanes[:].bitcast(I32), 0)
        make_identity(nc, ident[:])

        nc.sync.dma_start(out=x_sb[:], in_=x2)
        for quad in range(4):
            nc.scalar.dma_start(
                out=qplanes[32 * quad : 32 * quad + 16, 0:2048].bitcast(F32),
                in_=qsc[:, 4 * quad : 4 * quad + 4, 0:512],
            )
        for s in range(3):
            load_slab(s)
        nc.scalar.dma_start(out=brow[0:16, :], in_=qkv_b.rearrange("(r c) -> r c", c=512))
        nc.scalar.dma_start(out=brow[16:20, :], in_=proj_b.rearrange("(r c) -> r c", c=512))
        nc.scalar.dma_start(out=lb[:], in_=lunchbox.rearrange("(g p t) r -> p g (t r)", g=4, p=128, t=4))
        for lo, hi in ((2048, 4096), (4096, 8192)):
            for quad in range(4):
                nc.gpsimd.dma_start(
                    out=qplanes[32 * quad : 32 * quad + 16, lo:hi].bitcast(F32),
                    in_=qsc[:, 4 * quad : 4 * quad + 4, lo // 4 : hi // 4],
                )
        for s in range(8):
            load_proj_scales(s)
        for s in range(3, RING):
            load_slab(s)

        nc.vector.tensor_copy(out=identb[:], in_=ident[:])
        nc.vector.memset(qs[:], 0.0)
        nc.vector.tensor_reduce(
            out=mask4[:], in_=ident[:].rearrange("c (x a) -> c a x", a=4), axis=mybir.AxisListType.X, op=ADD
        )
        nc.vector.tensor_reduce(
            out=pick[:], in_=ident[:].rearrange("c (y z) -> c y z", z=4), axis=mybir.AxisListType.X, op=ADD
        )

        xwords = x_sb[:].bitcast(F32)
        xgw = xg[:].bitcast(F32)
        for a in range(2):
            xt = paux.tile([P, 512], F32, name="xt", tag="aux")
            for kl in range(2):
                kx = 2 * a + kl
                for u in range(2):
                    s = 2 * kl + u
                    nc.tensor.transpose(
                        xt[:, 128 * s : 128 * (s + 1)], xwords[:, 256 * kx + u : 256 * (kx + 1) : 2], ident[:]
                    )
            nc.scalar.copy(
                out=xgw[:, 512 * a : 512 * (a + 1)].rearrange("p (k n u) -> p k n u", k=2, u=2),
                in_=xt[:].rearrange("p (k u n) -> p k n u", k=2, u=2),
            )
        nc.vector.quantize_mx(out=xw[:].bitcast(FP8X4), scales=xs[:], in_=xg[:])

        bqp = paux.tile([P, 512], F32, name="bqp", tag="aux")
        for t in range(4):
            nc.tensor.matmul(
                out=bqp[:, 32 * t : 32 * (t + 1)], lhsT=brow[:, t:512:4], rhs=identb[:, 0:32], start=True, stop=True
            )
        nc.vector.tensor_scalar(
            out=bq128[:].rearrange("p (r t) -> p r t", t=4),
            in0=bqp[:, 0:128].rearrange("p (t r) -> p r t", t=4)[:, 0:8, :],
            scalar1=128.0,
            scalar2=None,
            op0=MULT,
        )
        for r in range(8, 20):
            bb = paux.tile([P, 512], F32, name="bb", tag="aux")
            nc.tensor.matmul(
                out=bb[:], lhsT=identb[:, r : r + 1].to_broadcast([P, P]), rhs=brow[:], start=True, stop=True
            )
            if r < 16:
                dst = bias_v[:, 512 * (r - 8) : 512 * (r - 7)].rearrange("n (t p) -> n t p", t=4)
                src = bb[:].rearrange("n (p t) -> n t p", t=4)
            else:
                dst = bias_o[:, 512 * (r - 16) : 512 * (r - 15)]
                src = bb[:]
            if r % 2 == 0:
                nc.scalar.copy(out=dst, in_=src)
            else:
                nc.vector.tensor_copy(out=dst, in_=src)
        nc.vector.tensor_reduce(
            out=lsum[:], in_=lb[:].rearrange("p g (t r) -> p (g t) r", r=32), axis=mybir.AxisListType.X, op=ADD
        )
        nc.vector.tensor_scalar(out=lscaled[:], in0=lsum[:], scalar1=SCALE, scalar2=None, op0=MULT)

        accs = {}
        hids = {}
        tps = {}
        rgs = {}
        rws = {}
        rss = {}
        acco = []

        def passes(grp, kx):
            s = 4 * grp + kx
            for g in range(4):
                if kx == 0:
                    acc = pacc.tile([P, 512], F32, name="acc", tag="acc")
                    accs[(grp, g)] = acc
                c16 = 4 * grp + g
                nc.tensor.matmul_mx(
                    out=accs[(grp, g)][:],
                    lhsT=xw[:, 128 * kx : 128 * (kx + 1)].bitcast(FP8X4),
                    lhsT_scale=xs[:, 128 * kx : 128 * (kx + 1)],
                    rhs=slabs[s][:, 2048 * g : 2048 * (g + 1)].bitcast(FP8X4),
                    rhs_scale=qplanes[4 * kx : 128, 512 * c16 : 512 * (c16 + 1)],
                    start=(kx == 0),
                    stop=(kx == 3),
                )
            if s + RING < 24:
                load_slab(s + RING)

        def q_tile(i, g):
            acc = pacc.tile([P, 512], F32, name="acc", tag="acc")
            c16 = 4 * i + g
            for u in range(4):
                for kx in range(4):
                    nc.tensor.matmul_mx(
                        out=acc[:, 128 * u : 128 * (u + 1)],
                        lhsT=slabs[4 * i + kx][:, 2048 * g + 512 * u : 2048 * g + 512 * (u + 1)].bitcast(FP8X4),
                        lhsT_scale=qplanes[4 * kx : 128, 512 * c16 + 128 * u : 512 * c16 + 128 * (u + 1)],
                        rhs=xw[:, 128 * kx : 128 * (kx + 1)].bitcast(FP8X4),
                        rhs_scale=xs[:, 128 * kx : 128 * (kx + 1)],
                        start=(kx == 0),
                        stop=(kx == 3),
                    )
            nc.vector.tensor_reduce(
                out=qs[:, 4 * c16 : 4 * c16 + 4],
                in_=acc[:].rearrange("p (u n) -> p u n", u=4),
                axis=mybir.AxisListType.X,
                op=ADD,
            )

        def factor():
            t1 = paux.tile([P, 512], F32, name="t1", tag="aux")
            nc.tensor.transpose(t1[:, 0:128], qs[:], ident[:])
            nc.scalar.copy(out=qst[:], in_=t1[:, 0:128])
            nc.vector.tensor_tensor(
                out=qsel[:].rearrange("c (t a b) -> c t a b", t=4, a=4),
                in0=qst[:].rearrange("c (b t) -> c t b", t=4).unsqueeze(2).to_broadcast([P, 4, 4, 32]),
                in1=mask4[:].unsqueeze(1).unsqueeze(3).to_broadcast([P, 4, 4, 32]),
                op=MULT,
            )
            s2 = paux.tile([P, 512], F32, name="s2", tag="aux")
            for t in range(4):
                nc.tensor.matmul(
                    out=s2[:, 8 * t : 8 * (t + 1)],
                    lhsT=qsel[:, 128 * t : 128 * (t + 1)],
                    rhs=pick[:, 0:8],
                    start=True,
                    stop=True,
                )
            nc.vector.tensor_tensor(
                out=qtot[:].rearrange("p (y t) -> p y t", t=4),
                in0=s2[:, 0:32].rearrange("p (t y) -> p y t", t=4),
                in1=bq128[:].rearrange("p (y t) -> p y t", t=4),
                op=ADD,
            )
            for i in range(2):
                sl = slice(16 * i, 16 * (i + 1))
                nc.vector.tensor_tensor(out=cvec[:, sl], in0=qtot[:, sl], in1=lscaled[:], op=MULT)

        def evac1(i, g):
            hid = hpool.tile([P, 512], F32, name="hid", tag="hid")
            c = 4 * i + g
            nc.vector.tensor_tensor(
                out=hid[:].rearrange("n (t p) -> n t p", t=4),
                in0=accs[(2 + i, g)][:].rearrange("n (p t) -> n t p", t=4),
                in1=bias_v[:, 512 * c : 512 * (c + 1)].rearrange("n (t p) -> n t p", t=4),
                op=ADD,
            )
            hids[(2 + i, g)] = hid

        def transposes(i, g):
            tp = paux.tile([P, 512], F32, name="tp", tag="aux")
            for t in range(4):
                nc.tensor.transpose(
                    tp[:, 128 * t : 128 * (t + 1)], hids[(2 + i, g)][:, 128 * t : 128 * (t + 1)], ident[:]
                )
            tps[(i, g)] = tp

        def evac2(i, g):
            if i == 0:
                rg = rpool.tile([P, 2, 2, 64, 4], BF16, name="rg", tag="rg", align_bytes=64)
                rw = rpool.tile([P, 256], U32, name="rw", tag="rw", align_bytes=64)
                rs = rpool.tile([P, 256], U8, name="rs", tag="rs", align_bytes=64)
                rgs[g] = rg
                rws[g] = rw
                rss[g] = rs
            c = 4 * i + g
            nc.vector.tensor_tensor(
                out=rgs[g][:, :, i, :, :],
                in0=tps[(i, g)][:].rearrange("p (t m j) -> p j m t", t=4, j=2),
                in1=cvec[:, 4 * c : 4 * c + 4].unsqueeze(1).unsqueeze(1).to_broadcast([P, 2, 64, 4]),
                op=MULT,
            )

        def quantise(i, g):
            for j in range(2):
                sl = slice(128 * j + 64 * i, 128 * j + 64 * (i + 1))
                nc.vector.quantize_mx(
                    out=rws[g][:, sl].bitcast(FP8X4),
                    scales=rss[g][:, sl],
                    in_=rgs[g][:, j, i, :, :].rearrange("p m t -> p (m t)"),
                )

        def mx2(ct, g, j, wbytes):
            nc.tensor.matmul_mx(
                out=acco[ct][:],
                lhsT=rws[g][:, 128 * j : 128 * (j + 1)].bitcast(FP8X4),
                lhsT_scale=rss[g][:, 128 * j : 128 * (j + 1)],
                rhs=wbytes.bitcast(FP8X4),
                rhs_scale=pplanes[4 * g : 128, 2048 * j + 512 * ct : 2048 * j + 512 * (ct + 1)],
                start=(g == 0 and j == 0),
                stop=(g == 3 and j == 1),
            )

        accd = []

        def mxd(g, j, wbytes, h):
            nc.tensor.matmul_mx(
                out=accd[h][:, 0:256],
                lhsT=rws[g][:, 128 * j : 128 * (j + 1)].bitcast(FP8X4),
                lhsT_scale=rss[g][:, 128 * j : 128 * (j + 1)],
                rhs=wbytes.bitcast(FP8X4),
                rhs_scale=pplanes[4 * g : 128, 2048 * j + 1536 + 256 * h : 2048 * j + 1536 + 256 * (h + 1)],
                start=(g == 0 and j == 0),
                stop=(g == 3 and j == 1),
            )

        def proj(g, j, tiles=3):
            for ct in range(tiles):
                if g == 0 and j == 0:
                    acc = pacc.tile([P, 512], F32, name="acc", tag="acc")
                    acco.append(acc)
                mx2(ct, g, j, slabs[16 + 2 * g + j][:, 2048 * ct : 2048 * (ct + 1)])

        for i in range(2):
            for g in range(4):
                q_tile(i, g)
            for kx in range(4):
                load_slab(4 * i + kx + RING)
        factor()
        for kx in range(4):
            passes(2, kx)
        for g in range(4):
            evac1(0, g)
        passes(3, 0)
        transposes(0, 0)
        transposes(0, 1)
        evac2(0, 0)
        evac2(0, 1)
        quantise(0, 0)
        quantise(0, 1)
        passes(3, 1)
        transposes(0, 2)
        transposes(0, 3)
        evac2(0, 2)
        evac2(0, 3)
        quantise(0, 2)
        quantise(0, 3)
        passes(3, 2)
        passes(3, 3)
        evac1(1, 0)
        evac1(1, 1)
        transposes(1, 0)
        evac2(1, 0)
        transposes(1, 1)
        evac1(1, 2)
        quantise(1, 0)
        evac2(1, 1)
        transposes(1, 2)
        evac1(1, 3)
        quantise(1, 1)
        evac2(1, 2)
        proj(0, 0)
        proj(0, 1)
        transposes(1, 3)
        quantise(1, 2)
        evac2(1, 3)
        quantise(1, 3)
        proj(1, 0)
        proj(1, 1)
        proj(2, 0)
        d0 = pacc.tile([P, 512], F32, name="acc", tag="acc")
        d1 = paux.tile([P, 512], F32, name="d1", tag="aux")
        accd.append(d0)
        accd.append(d1)
        for g, j in ((0, 0), (0, 1), (1, 0), (1, 1), (2, 0)):
            for h in range(2):
                mxd(g, j, slabs[16 + 2 * g + j][:, 6144 + 1024 * h : 6144 + 1024 * (h + 1)], h)
        proj(2, 1)
        proj(3, 0)

        def finish(acc, c0, n):
            o_sb = opool.tile([P, 512], F32, name="o_sb", tag="o_sb")
            nc.vector.tensor_tensor(out=o_sb[:, 0:n], in0=acc[:, 0:n], in1=bias_o[:, c0 : c0 + n], op=ADD)
            nc.sync.dma_start(out=out2[:, c0 : c0 + n], in_=o_sb[:, 0:n])

        for ct in range(3):
            mx2(ct, 3, 1, pieces[ct][:])
            finish(acco[ct], 512 * ct, 512)
        for g, j in ((2, 1), (3, 0)):
            for h in range(2):
                mxd(g, j, slabs[16 + 2 * g + j][:, 6144 + 1024 * h : 6144 + 1024 * (h + 1)], h)
        for h in range(2):
            mxd(3, 1, pieces[3][:, 1024 * h : 1024 * (h + 1)], h)
            finish(accd[h], 1536 + 256 * h, 256)
